import numpy as np
import ml_dtypes


def mxq(x, axis, fmt="e4m3"):
    dtype, down = {"e4m3": (ml_dtypes.float8_e4m3fn, 7), "e5m2": (ml_dtypes.float8_e5m2, 14)}[fmt]
    v = np.moveaxis(np.asarray(x, np.float32).astype(ml_dtypes.bfloat16).astype(np.float64), axis, -1)
    blocks = v.reshape(v.shape[:-1] + (-1, 32))
    amax = np.abs(blocks).max(-1, keepdims=True)
    byte = np.maximum(np.where(amax > 0, np.frexp(amax)[1] - 1 + 127, 0) - down, 1)
    scale = np.exp2(byte - 127.0)
    codes = (blocks / scale).astype(np.float32).astype(dtype).astype(np.float64)
    return np.moveaxis((codes * scale).reshape(v.shape), -1, axis)


WIDE = False


def mx_kscale(k):
    if not WIDE:
        return np.ones(k)
    levels = np.array([10, -10, 5, -5, 0])
    a = np.random.permutation(np.resize(levels, k // 512 * 4)).reshape(k // 512, 4)
    idx = np.arange(k)
    return np.exp2(a[idx // 512, idx % 128 // 32])


BF16 = ml_dtypes.bfloat16


def bf(x):
    return np.asarray(x, np.float32).astype(BF16)


def f64(x):
    return np.asarray(x).astype(np.float64)


B, T, C, CO, HS, DW, DA, DV, DG = 4, 128, 2048, 2048, 64, 128, 128, 128, 256
H = C // HS
EPS_GN = 0.00064


def setup_inputs():
    n = np.random.standard_normal
    t = mx_kscale(C)
    return {
        "y": bf(n((B, T, C)) * 0.1),
        "r": bf(n((B, T, C))),
        "k": bf(n((B, T, C)) * 0.6),
        "v": bf(n((B, T, C)) * 0.8),
        "g_hid": bf(1.0 / (1.0 + np.exp(-n((B, T, DG))))),
        "g2": bf(n((DG, C)) * 2.0 / np.sqrt(DG) * t),
        "r_k": bf(n((H, HS)) * 0.2 - 0.04),
        "ln_g": bf(1.0 + n((C,)) * 0.1),
        "ln_b": bf(n((C,)) * 0.1),
        "W_o": bf(n((CO, C)) * 0.7 / np.sqrt(C) / t),
    }


def reference(y, r, k, v, g_hid, g2, r_k, ln_g, ln_b, W_o):
    yh = f64(y).reshape(B, T, H, HS)
    mu = np.mean(yh, axis=-1, keepdims=True)
    var = np.mean((yh - mu) ** 2, axis=-1, keepdims=True)
    yn = ((yh - mu) / np.sqrt(var + EPS_GN)).reshape(B, T, C)
    yn = yn * f64(ln_g) + f64(ln_b)
    rh = f64(r).reshape(B, T, H, HS)
    kh = f64(k).reshape(B, T, H, HS)
    vh = f64(v).reshape(B, T, H, HS)
    dot = np.sum(rh * kh * f64(r_k), axis=-1, keepdims=True)
    y2 = yn + (dot * vh).reshape(B, T, C)
    g = f64(g_hid) @ f64(g2)
    z = y2 * g
    return mxq(z, 2, "e4m3") @ mxq(f64(W_o), 1, "e4m3").T

@@ -1,0 +1,295 @@
+from contextlib import ExitStack
+
+import concourse.mybir as mybir
+from concourse.masks import make_identity
+
+F32 = mybir.dt.float32
+BF16 = mybir.dt.bfloat16
+U32 = mybir.dt.uint32
+U8 = mybir.dt.uint8
+FP8X4 = mybir.dt.float8_e4m3fn_x4
+ADD = mybir.AluOpType.add
+SUB = mybir.AluOpType.subtract
+MUL = mybir.AluOpType.mult
+IDENT = mybir.ActivationFunctionType.Identity
+COPY = mybir.ActivationFunctionType.Copy
+SQRT = mybir.ActivationFunctionType.Sqrt
+AX_X = mybir.AxisListType.X
+
+P = 128
+NT = 4
+C = 2048
+CO = 2048
+HS = 64
+H = C // HS
+NG = 4
+NB = 16
+EPS = 0.00064
+
+FLOPS = 2 * 512 * 2048 * 2048 + 2 * 512 * 256 * 2048
+
+LD_BUFS = 22
+PROD_ON_G = (False, True, True, True)
+G_CHUNK = 512
+W_COPY_ON_V = (False, False, False, True)
+O_COPY_ON_V = (False, False, False, True)
+WP_AT = {1: (1,), 2: (2,), 3: (3,), 5: (4,), 6: (5,), 8: (6,), 9: (7,)}
+X_AT = {4: ((0, 0),), 5: ((0, 1),), 7: ((0, 2),), 8: ((1, 0),), 9: ((1, 1), (1, 2)), 10: ((0, 3),), 11: ((1, 3),),
+        12: ((2, 0), (2, 1)), 13: ((2, 2), (2, 3))}
+
+
+def tile_full_tmix_params_pc_kernel(tc, y, r, k, v, g_hid, g2, r_k, ln_g, ln_b, W_o, out):
+    nc = tc.nc
+    with ExitStack() as ctx:
+        const = ctx.enter_context(tc.tile_pool(name="const", bufs=1))
+        ld = ctx.enter_context(tc.tile_pool(name="ld", bufs=LD_BUFS))
+        work = ctx.enter_context(tc.tile_pool(name="work", bufs=2))
+        psum = ctx.enter_context(tc.psum_pool(name="psum", bufs=1))
+
+        ident = const.tile([P, P], F32, name="ident")
+        make_identity(nc, ident[:])
+        ones = const.tile([P, P], BF16, name="ones")
+        nc.vector.memset(ones[:], 1.0)
+        lnraw = const.tile([P, 2 * P], BF16, name="lnraw")
+        nc.vector.memset(lnraw[:], 0.0)
+        wrow = ld.tile([P, C], BF16, name="wrow", tag="ld")
+        nc.vector.memset(wrow[:], 0.0)
+        nc.scalar.dma_start(out=wrow[0:1, :], in_=r_k.rearrange("(o h) i -> o (h i)", o=1))
+        nc.scalar.dma_start(out=lnraw[0:8, :], in_=ln_g.rearrange("(a b) -> a b", b=2 * P))
+        nc.scalar.dma_start(out=lnraw[8:16, :], in_=ln_b.rearrange("(a b) -> a b", b=2 * P))
+        ghraw = const.tile([P, NT * 256], BF16, name="ghraw")
+        nc.scalar.dma_start(out=ghraw[:].rearrange("t (b d) -> t b d", b=NT), in_=g_hid.rearrange("b t d -> t b d"))
+
+        def load(src, label):
+            t = ld.tile([P, C], BF16, name=label, tag="ld")
+            nc.sync.dma_start(out=t[:], in_=src)
+            return t
+
+        yt, rt, kt, vt, wr = {}, {}, {}, {}, {}
+        g2v = g2.rearrange("(q e) c -> e q c", e=2)
+
+        def load_w(wp):
+            for b2 in range(2):
+                row = 256 * wp + 128 * b2
+                wr[(wp, b2)] = load(W_o[row:row + 128, :], "w%d_%d" % (wp, b2))
+
+        yt[0] = load(y[0], "y0")
+        g2raw = (load(g2v[0], "g2r0"), load(g2v[1], "g2r1"))
+        rt[0] = load(r[0], "r0")
+        kt[0] = load(k[0], "k0")
+        load_w(0)
+        rt[1] = load(r[1], "r1")
+        kt[1] = load(k[1], "k1")
+        vt[0] = load(v[0], "v0")
+        load_w(1)
+        yt[1] = load(y[1], "y1")
+        load_w(2)
+        load_w(3)
+        vt[1] = load(v[1], "v1")
+        rt[2] = load(r[2], "r2")
+        kt[2] = load(k[2], "k2")
+        yt[2] = load(y[2], "y2")
+        load_w(4)
+        load_w(5)
+        vt[2] = load(v[2], "v2")
+        rt[3] = load(r[3], "r3")
+        kt[3] = load(k[3], "k3")
+        yt[3] = load(y[3], "y3")
+        load_w(6)
+        load_w(7)
+        vt[3] = load(v[3], "v3")
+
+        wb = const.tile([P, C], BF16, name="wb")
+        for j in range(4):
+            pw = psum.tile([P, 512], F32, name="pw%d" % j, tag=("W" if j < 2 else "O"), bufs=2)
+            nc.tensor.matmul(pw[:], lhsT=ones[:], rhs=wrow[:, 512 * j:512 * j + 512], start=True, stop=True)
+            nc.scalar.copy(out=wb[:, 512 * j:512 * j + 512], in_=pw[:])
+
+        pl = psum.tile([P, P], F32, name="pl", tag="A", bufs=2)
+        nc.tensor.transpose(pl[:], lnraw[:].bitcast(F32), ident[:])
+        lnw = const.tile([P, 16], F32, name="lnw")
+        nc.vector.tensor_copy(out=lnw[:], in_=pl[:, 0:16])
+        lnT = const.tile([P, 32], F32, name="lnT")
+        nc.vector.tensor_copy(out=lnT[:], in_=lnw[:].bitcast(BF16))
+
+        pg = psum.tile([P, 512], F32, name="pg", tag="A", bufs=2)
+        for m in range(NT):
+            nc.tensor.transpose(pg[:, P * m:P * m + P], ghraw[:].bitcast(F32)[:, P * m:P * m + P], ident[:])
+        ghT = const.tile([P, 2, 512], BF16, name="ghT")
+        nc.vector.tensor_copy(out=ghT[:], in_=pg[:].bitcast(BF16).rearrange("q (n e) -> q e n", e=2))
+
+        g2p = const.tile([P, 2, C], BF16, name="g2p")
+        for e in range(2):
+            nc.gpsimd.tensor_scalar(
+                out=g2p[:, e, :].rearrange("q (a f p) -> q a f p", a=8, f=2),
+                in0=g2raw[e][:].rearrange("q (a p f) -> q a f p", a=8, f=2),
+                scalar1=1.0, scalar2=0.0, op0=MUL, op1=ADD)
+
+        wc = const.tile([P, NG, CO], U32, name="wc", align_bytes=64)
+        ws = const.tile([P, NG, CO], U8, name="ws", align_bytes=64)
+        zc = const.tile([P, NT, 512], U32, name="zc", align_bytes=64)
+        zs = const.tile([P, NT, 512], U8, name="zs", align_bytes=64)
+
+        ab, dd, rks, sts = {}, {}, {}, {}
+
+        def bn(m, heads):
+            if m not in sts:
+                sts[m] = work.tile([P, H, 6], F32, name="st%d" % m, tag="st")
+            for h in heads:
+                nc.vector.bn_stats(out=sts[m][:, h, :], in_=yt[m][:, HS * h:HS * h + HS])
+
+        def stats(m):
+            st = sts[m]
+            pr = work.tile([P, H, 2], F32, name="pr%d" % m, tag="pr")
+            nc.vector.tensor_tensor(out=pr[:], in0=st[:, :, 1:3], in1=st[:, :, 4:6], op=ADD)
+            dm = work.tile([P, H], F32, name="dm%d" % m, tag="dm")
+            nc.vector.tensor_tensor(out=dm[:], in0=st[:, :, 1], in1=st[:, :, 4], op=SUB)
+            d2 = work.tile([P, H], F32, name="d2%d" % m, tag="d2")
+            nc.vector.tensor_tensor(out=d2[:], in0=dm[:], in1=dm[:], op=MUL)
+            qe = work.tile([P, H], F32, name="qe%d" % m, tag="qe")
+            nc.vector.tensor_scalar(out=qe[:], in0=pr[:, :, 1], scalar1=1.0 / HS, scalar2=EPS, op0=MUL, op1=ADD)
+            vv = work.tile([P, H], F32, name="vv%d" % m, tag="vv")
+            nc.vector.scalar_tensor_tensor(out=vv[:], in0=d2[:], scalar=0.25, in1=qe[:], op0=MUL, op1=ADD)
+            sd = work.tile([P, H], F32, name="sd%d" % m, tag="sd")
+            nc.scalar.activation(out=sd[:], in_=vv[:], func=SQRT)
+            a_b = work.tile([P, 2, H], F32, name="ab%d" % m, tag="ab")
+            nc.vector.reciprocal(out=a_b[:, 0, :], in_=sd[:])
+            nc.vector.scalar_tensor_tensor(out=a_b[:, 1, :], in0=pr[:, :, 0], scalar=-0.5, in1=a_b[:, 0, :], op0=MUL, op1=MUL)
+            ab[m] = a_b
+
+        def prod(m):
+            eng = nc.gpsimd if PROD_ON_G[m] else nc.vector
+            wid = G_CHUNK if PROD_ON_G[m] else C
+            rk = work.tile([P, C], F32, name="rk%d" % m, tag="rk")
+            for j in range(C // wid):
+                cs = slice(j * wid, (j + 1) * wid)
+                eng.tensor_tensor(out=rk[:, cs], in0=rt[m][:, cs], in1=kt[m][:, cs], op=MUL)
+            for j in range(C // wid):
+                cs = slice(j * wid, (j + 1) * wid)
+                eng.tensor_tensor(out=rk[:, cs], in0=rk[:, cs], in1=wb[:, cs], op=MUL)
+            rks[m] = rk
+            dd[m] = work.tile([P, H], F32, name="dd%d" % m, tag="dd")
+
+        def red(m, g):
+            nc.vector.tensor_reduce(out=dd[m][:, 8 * g:8 * g + 8],
+                                    in_=rks[m][:, 512 * g:512 * g + 512].rearrange("t (h i) -> t h i", i=HS),
+                                    axis=AX_X, op=ADD)
+
+        s12 = {}
+
+        def heads(m, g):
+            s1 = work.tile([P, 4, P], F32, name="s1_%d_%d" % (m, g), tag="s1", bufs=3)
+            s2 = work.tile([P, 4, P], F32, name="s2_%d_%d" % (m, g), tag="s2", bufs=3)
+            for u in range(2):
+                for hq in range(4):
+                    h = 8 * g + 4 * u + hq
+                    nc.scalar.activation(out=s1[:, 2 * u:2 * u + 2, 32 * hq:32 * hq + 32],
+                                         in_=yt[m][:, HS * h:HS * h + HS].rearrange("t (p e) -> t e p", e=2),
+                                         func=IDENT, bias=ab[m][:, 1, h:h + 1], scale=ab[m][:, 0, h:h + 1])
+            for u in range(2):
+                for hq in range(4):
+                    h = 8 * g + 4 * u + hq
+                    nc.scalar.activation(out=s2[:, 2 * u:2 * u + 2, 32 * hq:32 * hq + 32],
+                                         in_=vt[m][:, HS * h:HS * h + HS].rearrange("t (p e) -> t e p", e=2),
+                                         func=COPY, scale=dd[m][:, h:h + 1])
+            s12[(m, g)] = (s1, s2)
+
+        def unit(m, g):
+            s1, s2 = s12[(m, g)]
+            pa = psum.tile([P, 4, P], F32, name="pa%d_%d" % (m, g), tag="A", bufs=2)
+            for t in range(4):
+                nc.tensor.transpose(pa[:, t, :], s1[:, t, :], ident[:])
+            pb = psum.tile([P, 4, P], F32, name="pb%d_%d" % (m, g), tag="B", bufs=1)
+            for t in range(4):
+                nc.tensor.transpose(pb[:, t, :], s2[:, t, :], ident[:])
+            pgt = psum.tile([P, 4, P], F32, name="pgt%d_%d" % (m, g), tag="G", bufs=1)
+            for t in range(4):
+                blk = 4 * g + t
+                for e in range(2):
+                    nc.tensor.matmul(pgt[:, t, :], lhsT=g2p[:, e, P * blk:P * blk + P], rhs=ghT[:, e, P * m:P * m + P],
+                                     start=(e == 0), stop=(e == 1))
+            e1 = work.tile([P, 4, P], F32, name="e1_%d_%d" % (m, g), tag="e1", bufs=3)
+            for t in range(4):
+                blk = 4 * g + t
+                nc.scalar.activation(out=e1[:, t, :], in_=pa[:, t, :], func=IDENT,
+                                     bias=lnT[:, 16 + blk:17 + blk], scale=lnT[:, blk:blk + 1])
+            nc.vector.tensor_tensor(out=e1[:], in0=e1[:], in1=pb[:], op=ADD)
+            zg = work.tile([P, P, 4], BF16, name="zg%d_%d" % (m, g), tag="zg", bufs=3, align_bytes=64)
+            nc.vector.tensor_tensor(out=zg[:], in0=e1[:].rearrange("p t r -> p r t"), in1=pgt[:].rearrange("p t r -> p r t"), op=MUL)
+            nc.vector.quantize_mx(out=zc[:, m, P * g:P * g + P].bitcast(FP8X4), scales=zs[:, m, P * g:P * g + P],
+                                  in_=zg[:].rearrange("p r t -> p (r t)"))
+
+        def wpair(wp):
+            wg = work.tile([P, 4096], BF16, name="wg%d" % wp, tag="wg", bufs=2, align_bytes=64)
+            wgv = wg[:].bitcast(F32).rearrange("p (g c u) -> p g c u", g=NG, u=2)
+            for g in range(NG):
+                pw2 = psum.tile([P, 2, 256], F32, name="pw%d_%d" % (wp, g), tag="W", bufs=2)
+                for u in range(2):
+                    for b2 in range(2):
+                        col = 256 * g + 128 * u
+                        nc.tensor.transpose(pw2[:, u, P * b2:P * b2 + P], wr[(wp, b2)][:].bitcast(F32)[:, col:col + P], ident[:])
+                if W_COPY_ON_V[g]:
+                    nc.vector.tensor_copy(out=wgv[:, g, :, :], in_=pw2[:].rearrange("p u c -> p c u"))
+                else:
+                    nc.scalar.copy(out=wgv[:, g, :, :], in_=pw2[:].rearrange("p u c -> p c u"))
+            for g in range(NG):
+                nc.vector.quantize_mx(out=wc[:, g, 256 * wp:256 * wp + 256].bitcast(FP8X4), scales=ws[:, g, 256 * wp:256 * wp + 256],
+                                      in_=wg[:, 1024 * g:1024 * g + 1024])
+
+        def mx_pass(po, m, n, g):
+            nc.tensor.matmul_mx(out=po[:], lhsT=zc[:, m, P * g:P * g + P].bitcast(FP8X4), lhsT_scale=zs[:, m, P * g:P * g + P],
+                                rhs=wc[:, g, 512 * n:512 * n + 512].bitcast(FP8X4), rhs_scale=ws[:, g, 512 * n:512 * n + 512],
+                                start=(g == 0), stop=(g == NG - 1))
+
+        def drain(po, m, n):
+            ob = work.tile([P, 512], F32, name="ob%d_%d" % (m, n), tag="ob", bufs=4)
+            if O_COPY_ON_V[n]:
+                nc.vector.tensor_copy(out=ob[:], in_=po[:])
+            else:
+                nc.scalar.copy(out=ob[:], in_=po[:])
+            nc.sync.dma_start(out=out[m, :, 512 * n:512 * n + 512], in_=ob[:])
+
+        def xgroup(m, n):
+            po = psum.tile([P, 512], F32, name="po%d_%d" % (m, n), tag="O", bufs=2)
+            for g in range(NG):
+                mx_pass(po, m, n, g)
+            drain(po, m, n)
+
+        bn(0, range(H))
+        stats(0)
+        prod(0)
+        wpair(0)
+        for g in range(NG):
+            red(0, g)
+        for m in range(1, NT):
+            prod(m)
+        heads(0, 0)
+        last = {}
+        for s in range(16):
+            m, g = divmod(s, 4)
+            if m + 1 < NT:
+                bn(m + 1, range(8 * g, 8 * g + 8))
+                red(m + 1, g)
+                if g == 3:
+                    stats(m + 1)
+            if s + 1 < 16:
+                heads((s + 1) // 4, (s + 1) % 4)
+            unit(m, g)
+            for wp in WP_AT.get(s, ()):
+                wpair(wp)
+            for (xm, xn) in X_AT.get(s, ()):
+                xgroup(xm, xn)
+            if m == NT - 1:
+                for n in range(2):
+                    if g == 0:
+                        last[n] = psum.tile([P, 512], F32, name="plast%d" % n, tag="W", bufs=2)
+                    mx_pass(last[n], m, n, g)
+                for n in range(2, 4):
+                    if g == 2:
+                        last[n] = psum.tile([P, 512], F32, name="plast%d" % n, tag="O", bufs=2)
+                        mx_pass(last[n], m, n, 0)
+                        mx_pass(last[n], m, n, 1)
+                    if g >= 2:
+                        mx_pass(last[n], m, n, g)
+        for n in range(4):
+            drain(last[n], NT - 1, n)

@@ -23,19 +23,15 @@ CO = 2048
 HS = 64
 H = C // HS
 NG = 4
-NB = 16
 EPS = 0.00064
 
 FLOPS = 2 * 512 * 2048 * 2048 + 2 * 512 * 256 * 2048
 
 LD_BUFS = 22
+PINNED = True
 PROD_ON_G = (False, True, True, True)
-G_CHUNK = 512
-W_COPY_ON_V = (False, False, False, True)
-O_COPY_ON_V = (False, False, False, True)
-WP_AT = {1: (1,), 2: (2,), 3: (3,), 5: (4,), 6: (5,), 8: (6,), 9: (7,)}
-X_AT = {4: ((0, 0),), 5: ((0, 1),), 7: ((0, 2),), 8: ((1, 0),), 9: ((1, 1), (1, 2)), 10: ((0, 3),), 11: ((1, 3),),
-        12: ((2, 0), (2, 1)), 13: ((2, 2), (2, 3))}
+BN_AT = {0: ((1, 0, 16),), 1: ((1, 16, 32),), 2: ((2, 0, 8),), 3: ((2, 8, 16),), 4: ((2, 16, 24),), 5: ((2, 24, 32),),
+         6: ((3, 0, 8),), 7: ((3, 8, 16),), 8: ((3, 16, 24),), 9: ((3, 24, 32),)}
 
 
 def tile_full_tmix_params_pc_kernel(tc, y, r, k, v, g_hid, g2, r_k, ln_g, ln_b, W_o, out):
@@ -45,20 +41,20 @@ def tile_full_tmix_params_pc_kernel(tc, y, r, k, v, g_hid, g2, r_k, ln_g, ln_b, 
         ld = ctx.enter_context(tc.tile_pool(name="ld", bufs=LD_BUFS))
         work = ctx.enter_context(tc.tile_pool(name="work", bufs=2))
         psum = ctx.enter_context(tc.psum_pool(name="psum", bufs=1))
+        if PINNED:
+            ctx.enter_context(tc.manual_schedule())
 
         ident = const.tile([P, P], F32, name="ident")
         make_identity(nc, ident[:])
-        ones = const.tile([P, P], BF16, name="ones")
-        nc.vector.memset(ones[:], 1.0)
-        lnraw = const.tile([P, 2 * P], BF16, name="lnraw")
-        nc.vector.memset(lnraw[:], 0.0)
         wrow = ld.tile([P, C], BF16, name="wrow", tag="ld")
         nc.vector.memset(wrow[:], 0.0)
-        nc.scalar.dma_start(out=wrow[0:1, :], in_=r_k.rearrange("(o h) i -> o (h i)", o=1))
-        nc.scalar.dma_start(out=lnraw[0:8, :], in_=ln_g.rearrange("(a b) -> a b", b=2 * P))
-        nc.scalar.dma_start(out=lnraw[8:16, :], in_=ln_b.rearrange("(a b) -> a b", b=2 * P))
+        lnraw = const.tile([P, 2 * P], BF16, name="lnraw")
+        nc.vector.memset(lnraw[:], 0.0)
+        lnrawb = const.tile([P, 2 * P], BF16, name="lnrawb")
+        nc.vector.memset(lnrawb[:], 0.0)
+        ones = const.tile([P, P], BF16, name="ones")
+        nc.vector.memset(ones[:], 1.0)
         ghraw = const.tile([P, NT * 256], BF16, name="ghraw")
-        nc.scalar.dma_start(out=ghraw[:].rearrange("t (b d) -> t b d", b=NT), in_=g_hid.rearrange("b t d -> t b d"))
 
         def load(src, label):
             t = ld.tile([P, C], BF16, name=label, tag="ld")
@@ -73,64 +69,70 @@ def tile_full_tmix_params_pc_kernel(tc, y, r, k, v, g_hid, g2, r_k, ln_g, ln_b, 
                 row = 256 * wp + 128 * b2
                 wr[(wp, b2)] = load(W_o[row:row + 128, :], "w%d_%d" % (wp, b2))
 
+        def load_rk(m):
+            rt[m] = load(r[m], "r%d" % m)
+            kt[m] = load(k[m], "k%d" % m)
+
         yt[0] = load(y[0], "y0")
+        load_rk(0)
+        nc.sync.dma_start(out=wrow[0:1, :], in_=r_k.rearrange("(o h) i -> o (h i)", o=1))
+        nc.sync.dma_start(out=ghraw[:].rearrange("t (b d) -> t b d", b=NT), in_=g_hid.rearrange("b t d -> t b d"))
+        nc.sync.dma_start(out=lnraw[0:8, :], in_=ln_g.rearrange("(a b) -> a b", b=2 * P))
+        nc.sync.dma_start(out=lnrawb[0:8, :], in_=ln_b.rearrange("(a b) -> a b", b=2 * P))
         g2raw = (load(g2v[0], "g2r0"), load(g2v[1], "g2r1"))
-        rt[0] = load(r[0], "r0")
-        kt[0] = load(k[0], "k0")
-        load_w(0)
-        rt[1] = load(r[1], "r1")
-        kt[1] = load(k[1], "k1")
         vt[0] = load(v[0], "v0")
-        load_w(1)
+        load_rk(1)
         yt[1] = load(y[1], "y1")
+        load_w(0)
+        load_w(1)
+        vt[1] = load(v[1], "v1")
         load_w(2)
         load_w(3)
-        vt[1] = load(v[1], "v1")
-        rt[2] = load(r[2], "r2")
-        kt[2] = load(k[2], "k2")
+        load_rk(2)
         yt[2] = load(y[2], "y2")
         load_w(4)
         load_w(5)
         vt[2] = load(v[2], "v2")
-        rt[3] = load(r[3], "r3")
-        kt[3] = load(k[3], "k3")
+        load_rk(3)
         yt[3] = load(y[3], "y3")
         load_w(6)
         load_w(7)
         vt[3] = load(v[3], "v3")
 
         wb = const.tile([P, C], BF16, name="wb")
-        for j in range(4):
-            pw = psum.tile([P, 512], F32, name="pw%d" % j, tag=("W" if j < 2 else "O"), bufs=2)
-            nc.tensor.matmul(pw[:], lhsT=ones[:], rhs=wrow[:, 512 * j:512 * j + 512], start=True, stop=True)
-            nc.scalar.copy(out=wb[:, 512 * j:512 * j + 512], in_=pw[:])
-
-        pl = psum.tile([P, P], F32, name="pl", tag="A", bufs=2)
-        nc.tensor.transpose(pl[:], lnraw[:].bitcast(F32), ident[:])
         lnw = const.tile([P, 16], F32, name="lnw")
-        nc.vector.tensor_copy(out=lnw[:], in_=pl[:, 0:16])
         lnT = const.tile([P, 32], F32, name="lnT")
-        nc.vector.tensor_copy(out=lnT[:], in_=lnw[:].bitcast(BF16))
-
-        pg = psum.tile([P, 512], F32, name="pg", tag="A", bufs=2)
-        for m in range(NT):
-            nc.tensor.transpose(pg[:, P * m:P * m + P], ghraw[:].bitcast(F32)[:, P * m:P * m + P], ident[:])
         ghT = const.tile([P, 2, 512], BF16, name="ghT")
-        nc.vector.tensor_copy(out=ghT[:], in_=pg[:].bitcast(BF16).rearrange("q (n e) -> q e n", e=2))
-
         g2p = const.tile([P, 2, C], BF16, name="g2p")
-        for e in range(2):
-            nc.gpsimd.tensor_scalar(
-                out=g2p[:, e, :].rearrange("q (a f p) -> q a f p", a=8, f=2),
-                in0=g2raw[e][:].rearrange("q (a p f) -> q a f p", a=8, f=2),
-                scalar1=1.0, scalar2=0.0, op0=MUL, op1=ADD)
-
         wc = const.tile([P, NG, CO], U32, name="wc", align_bytes=64)
         ws = const.tile([P, NG, CO], U8, name="ws", align_bytes=64)
         zc = const.tile([P, NT, 512], U32, name="zc", align_bytes=64)
         zs = const.tile([P, NT, 512], U8, name="zs", align_bytes=64)
 
-        ab, dd, rks, sts = {}, {}, {}, {}
+        def setup_wb(js):
+            for j in js:
+                pw = psum.tile([P, 512], F32, name="pwb%d" % j, tag=("W" if j < 2 else "O"), bufs=(3 if j < 2 else 2))
+                nc.tensor.matmul(pw[:], lhsT=ones[:], rhs=wrow[:, 512 * j:512 * j + 512], start=True, stop=True)
+                nc.scalar.copy(out=wb[:, 512 * j:512 * j + 512], in_=pw[:])
+
+        def setup_ln_gh():
+            pl = psum.tile([P, 2, P], F32, name="pl", tag="B", bufs=1)
+            nc.tensor.transpose(pl[:, 0, :], lnraw[:].bitcast(F32), ident[:])
+            nc.tensor.transpose(pl[:, 1, :], lnrawb[:].bitcast(F32), ident[:])
+            nc.vector.tensor_copy(out=lnw[:].rearrange("p (a b) -> p a b", a=2), in_=pl[:, :, 0:8])
+            nc.vector.tensor_copy(out=lnT[:], in_=lnw[:].bitcast(BF16))
+            pg = psum.tile([P, 512], F32, name="pg", tag="G", bufs=1)
+            for m in range(NT):
+                nc.tensor.transpose(pg[:, P * m:P * m + P], ghraw[:].bitcast(F32)[:, P * m:P * m + P], ident[:])
+            nc.vector.tensor_copy(out=ghT[:], in_=pg[:].bitcast(BF16).rearrange("q (n e) -> q e n", e=2))
+
+        def setup_g2p(g):
+            for e in range(2):
+                nc.scalar.copy(out=g2p[:, e, 512 * g:512 * g + 512].rearrange("q (a f p) -> q a f p", a=2, f=2),
+                               in_=g2raw[e][:, 512 * g:512 * g + 512].rearrange("q (a p f) -> q a f p", a=2, f=2))
+
+        prs, vvs, sds = {}, {}, {}
+        ab, dd, rks, sts, s1s, s2s, pas, pbs, pgs, e1s, zgs, wgs, pws, pos = {}, {}, {}, {}, {}, {}, {}, {}, {}, {}, {}, {}, {}, {}
 
         def bn(m, heads):
             if m not in sts:
@@ -144,152 +146,241 @@ def tile_full_tmix_params_pc_kernel(tc, y, r, k, v, g_hid, g2, r_k, ln_g, ln_b, 
             nc.vector.tensor_tensor(out=pr[:], in0=st[:, :, 1:3], in1=st[:, :, 4:6], op=ADD)
             dm = work.tile([P, H], F32, name="dm%d" % m, tag="dm")
             nc.vector.tensor_tensor(out=dm[:], in0=st[:, :, 1], in1=st[:, :, 4], op=SUB)
-            d2 = work.tile([P, H], F32, name="d2%d" % m, tag="d2")
-            nc.vector.tensor_tensor(out=d2[:], in0=dm[:], in1=dm[:], op=MUL)
             qe = work.tile([P, H], F32, name="qe%d" % m, tag="qe")
             nc.vector.tensor_scalar(out=qe[:], in0=pr[:, :, 1], scalar1=1.0 / HS, scalar2=EPS, op0=MUL, op1=ADD)
+            d2 = work.tile([P, H], F32, name="d2%d" % m, tag="d2")
+            nc.vector.tensor_tensor(out=d2[:], in0=dm[:], in1=dm[:], op=MUL)
             vv = work.tile([P, H], F32, name="vv%d" % m, tag="vv")
             nc.vector.scalar_tensor_tensor(out=vv[:], in0=d2[:], scalar=0.25, in1=qe[:], op0=MUL, op1=ADD)
-            sd = work.tile([P, H], F32, name="sd%d" % m, tag="sd")
-            nc.scalar.activation(out=sd[:], in_=vv[:], func=SQRT)
-            a_b = work.tile([P, 2, H], F32, name="ab%d" % m, tag="ab")
-            nc.vector.reciprocal(out=a_b[:, 0, :], in_=sd[:])
-            nc.vector.scalar_tensor_tensor(out=a_b[:, 1, :], in0=pr[:, :, 0], scalar=-0.5, in1=a_b[:, 0, :], op0=MUL, op1=MUL)
-            ab[m] = a_b
+            prs[m] = pr
+            vvs[m] = vv
 
-        def prod(m):
+        def stats_s(m):
+            sds[m] = work.tile([P, H], F32, name="sd%d" % m, tag="sd")
+            nc.scalar.activation(out=sds[m][:], in_=vvs[m][:], func=SQRT)
+
+        def stats_b(m):
+            ab[m] = work.tile([P, 2, H], F32, name="ab%d" % m, tag="ab")
+            nc.vector.reciprocal(out=ab[m][:, 0, :], in_=sds[m][:])
+            nc.vector.scalar_tensor_tensor(out=ab[m][:, 1, :], in0=prs[m][:, :, 0], scalar=-0.5, in1=ab[m][:, 0, :], op0=MUL, op1=MUL)
+
+        def prod(m, g):
             eng = nc.gpsimd if PROD_ON_G[m] else nc.vector
-            wid = G_CHUNK if PROD_ON_G[m] else C
-            rk = work.tile([P, C], F32, name="rk%d" % m, tag="rk")
-            for j in range(C // wid):
-                cs = slice(j * wid, (j + 1) * wid)
-                eng.tensor_tensor(out=rk[:, cs], in0=rt[m][:, cs], in1=kt[m][:, cs], op=MUL)
-            for j in range(C // wid):
-                cs = slice(j * wid, (j + 1) * wid)
-                eng.tensor_tensor(out=rk[:, cs], in0=rk[:, cs], in1=wb[:, cs], op=MUL)
-            rks[m] = rk
-            dd[m] = work.tile([P, H], F32, name="dd%d" % m, tag="dd")
+            if m not in rks:
+                rks[m] = work.tile([P, C], F32, name="rk%d" % m, tag="rk")
+                dd[m] = work.tile([P, H], F32, name="dd%d" % m, tag="dd")
+            cs = slice(512 * g, 512 * g + 512)
+            eng.tensor_tensor(out=rks[m][:, cs], in0=rt[m][:, cs], in1=kt[m][:, cs], op=MUL)
+            eng.tensor_tensor(out=rks[m][:, cs], in0=rks[m][:, cs], in1=wb[:, cs], op=MUL)
 
         def red(m, g):
             nc.vector.tensor_reduce(out=dd[m][:, 8 * g:8 * g + 8],
                                     in_=rks[m][:, 512 * g:512 * g + 512].rearrange("t (h i) -> t h i", i=HS),
                                     axis=AX_X, op=ADD)
 
-        s12 = {}
+        def heads_a(j):
+            m, g = divmod(j, 4)
+            s1s[j] = work.tile([P, 4, P], F32, name="s1_%d" % j, tag="s1", bufs=3)
+            for hh in range(8):
+                h = 8 * g + hh
+                u, hq = divmod(hh, 4)
+                nc.scalar.activation(out=s1s[j][:, 2 * u:2 * u + 2, 32 * hq:32 * hq + 32],
+                                     in_=yt[m][:, HS * h:HS * h + HS].rearrange("t (p e) -> t e p", e=2),
+                                     func=IDENT, bias=ab[m][:, 1, h:h + 1], scale=ab[m][:, 0, h:h + 1])
 
-        def heads(m, g):
-            s1 = work.tile([P, 4, P], F32, name="s1_%d_%d" % (m, g), tag="s1", bufs=3)
-            s2 = work.tile([P, 4, P], F32, name="s2_%d_%d" % (m, g), tag="s2", bufs=3)
-            for u in range(2):
-                for hq in range(4):
-                    h = 8 * g + 4 * u + hq
-                    nc.scalar.activation(out=s1[:, 2 * u:2 * u + 2, 32 * hq:32 * hq + 32],
-                                         in_=yt[m][:, HS * h:HS * h + HS].rearrange("t (p e) -> t e p", e=2),
-                                         func=IDENT, bias=ab[m][:, 1, h:h + 1], scale=ab[m][:, 0, h:h + 1])
-            for u in range(2):
-                for hq in range(4):
-                    h = 8 * g + 4 * u + hq
-                    nc.scalar.activation(out=s2[:, 2 * u:2 * u + 2, 32 * hq:32 * hq + 32],
-                                         in_=vt[m][:, HS * h:HS * h + HS].rearrange("t (p e) -> t e p", e=2),
-                                         func=COPY, scale=dd[m][:, h:h + 1])
-            s12[(m, g)] = (s1, s2)
+        def heads_b(j):
+            m, g = divmod(j, 4)
+            s2s[j] = work.tile([P, 4, P], F32, name="s2_%d" % j, tag="s2", bufs=3)
+            for hh in range(8):
+                h = 8 * g + hh
+                u, hq = divmod(hh, 4)
+                nc.scalar.activation(out=s2s[j][:, 2 * u:2 * u + 2, 32 * hq:32 * hq + 32],
+                                     in_=vt[m][:, HS * h:HS * h + HS].rearrange("t (p e) -> t e p", e=2),
+                                     func=COPY, scale=dd[m][:, h:h + 1])
 
-        def unit(m, g):
-            s1, s2 = s12[(m, g)]
-            pa = psum.tile([P, 4, P], F32, name="pa%d_%d" % (m, g), tag="A", bufs=2)
+        def tr_a(j):
+            pas[j] = psum.tile([P, 4, P], F32, name="pa%d" % j, tag="A", bufs=1)
             for t in range(4):
-                nc.tensor.transpose(pa[:, t, :], s1[:, t, :], ident[:])
-            pb = psum.tile([P, 4, P], F32, name="pb%d_%d" % (m, g), tag="B", bufs=1)
+                nc.tensor.transpose(pas[j][:, t, :], s1s[j][:, t, :], ident[:])
+
+        def tr_b(j):
+            pbs[j] = psum.tile([P, 4, P], F32, name="pb%d" % j, tag="B", bufs=1)
             for t in range(4):
-                nc.tensor.transpose(pb[:, t, :], s2[:, t, :], ident[:])
-            pgt = psum.tile([P, 4, P], F32, name="pgt%d_%d" % (m, g), tag="G", bufs=1)
-            for t in range(4):
+                nc.tensor.transpose(pbs[j][:, t, :], s2s[j][:, t, :], ident[:])
+
+        def gate(j, t):
+            m, g = divmod(j, 4)
+            if t == 0:
+                pgs[j] = psum.tile([P, 4, P], F32, name="pg%d" % j, tag="G", bufs=1)
+            if True:
                 blk = 4 * g + t
                 for e in range(2):
-                    nc.tensor.matmul(pgt[:, t, :], lhsT=g2p[:, e, P * blk:P * blk + P], rhs=ghT[:, e, P * m:P * m + P],
+                    nc.tensor.matmul(pgs[j][:, t, :], lhsT=g2p[:, e, P * blk:P * blk + P], rhs=ghT[:, e, P * m:P * m + P],
                                      start=(e == 0), stop=(e == 1))
-            e1 = work.tile([P, 4, P], F32, name="e1_%d_%d" % (m, g), tag="e1", bufs=3)
+
+        def e_one(j):
+            g = j % 4
+            e1s[j] = work.tile([P, 4, P], F32, name="e1_%d" % j, tag="e1", bufs=3)
             for t in range(4):
                 blk = 4 * g + t
-                nc.scalar.activation(out=e1[:, t, :], in_=pa[:, t, :], func=IDENT,
+                nc.scalar.activation(out=e1s[j][:, t, :], in_=pas[j][:, t, :], func=IDENT,
                                      bias=lnT[:, 16 + blk:17 + blk], scale=lnT[:, blk:blk + 1])
-            nc.vector.tensor_tensor(out=e1[:], in0=e1[:], in1=pb[:], op=ADD)
-            zg = work.tile([P, P, 4], BF16, name="zg%d_%d" % (m, g), tag="zg", bufs=3, align_bytes=64)
-            nc.vector.tensor_tensor(out=zg[:], in0=e1[:].rearrange("p t r -> p r t"), in1=pgt[:].rearrange("p t r -> p r t"), op=MUL)
-            nc.vector.quantize_mx(out=zc[:, m, P * g:P * g + P].bitcast(FP8X4), scales=zs[:, m, P * g:P * g + P],
-                                  in_=zg[:].rearrange("p r t -> p (r t)"))
 
-        def wpair(wp):
-            wg = work.tile([P, 4096], BF16, name="wg%d" % wp, tag="wg", bufs=2, align_bytes=64)
-            wgv = wg[:].bitcast(F32).rearrange("p (g c u) -> p g c u", g=NG, u=2)
-            for g in range(NG):
-                pw2 = psum.tile([P, 2, 256], F32, name="pw%d_%d" % (wp, g), tag="W", bufs=2)
-                for u in range(2):
-                    for b2 in range(2):
-                        col = 256 * g + 128 * u
-                        nc.tensor.transpose(pw2[:, u, P * b2:P * b2 + P], wr[(wp, b2)][:].bitcast(F32)[:, col:col + P], ident[:])
-                if W_COPY_ON_V[g]:
-                    nc.vector.tensor_copy(out=wgv[:, g, :, :], in_=pw2[:].rearrange("p u c -> p c u"))
-                else:
-                    nc.scalar.copy(out=wgv[:, g, :, :], in_=pw2[:].rearrange("p u c -> p c u"))
+        def add_mul(j):
+            nc.vector.tensor_tensor(out=e1s[j][:], in0=e1s[j][:], in1=pbs[j][:], op=ADD)
+            zgs[j] = work.tile([P, P, 4], BF16, name="zg%d" % j, tag="zg", bufs=3, align_bytes=64)
+            nc.vector.tensor_tensor(out=zgs[j][:], in0=e1s[j][:].rearrange("p t r -> p r t"),
+                                    in1=pgs[j][:].rearrange("p t r -> p r t"), op=MUL)
+
+        def zq(j):
+            m, g = divmod(j, 4)
+            nc.vector.quantize_mx(out=zc[:, m, P * g:P * g + P].bitcast(FP8X4), scales=zs[:, m, P * g:P * g + P],
+                                  in_=zgs[j][:].rearrange("p r t -> p (r t)"))
+
+        def w_tr(kk):
+            wp, g = divmod(kk, 4)
+            pws[kk] = psum.tile([P, 2, 256], F32, name="pw%d" % kk, tag="W", bufs=3)
+            for u in range(2):
+                for b2 in range(2):
+                    col = 256 * g + 128 * u
+                    nc.tensor.transpose(pws[kk][:, u, P * b2:P * b2 + P], wr[(wp, b2)][:].bitcast(F32)[:, col:col + P], ident[:])
+
+        def w_copy(kk):
+            wp, g = divmod(kk, 4)
+            if g == 0:
+                wgs[wp] = work.tile([P, 4096], BF16, name="wg%d" % wp, tag="wg", bufs=2, align_bytes=64)
+            dst = wgs[wp][:].bitcast(F32).rearrange("p (g c u) -> p g c u", g=NG, u=2)[:, g, :, :]
+            if kk % 4 == 3:
+                nc.vector.tensor_copy(out=dst, in_=pws[kk][:].rearrange("p u c -> p c u"))
+            else:
+                nc.scalar.copy(out=dst, in_=pws[kk][:].rearrange("p u c -> p c u"))
+
+        def w_q(wp):
             for g in range(NG):
                 nc.vector.quantize_mx(out=wc[:, g, 256 * wp:256 * wp + 256].bitcast(FP8X4), scales=ws[:, g, 256 * wp:256 * wp + 256],
-                                      in_=wg[:, 1024 * g:1024 * g + 1024])
+                                      in_=wgs[wp][:, 1024 * g:1024 * g + 1024])
 
-        def mx_pass(po, m, n, g):
-            nc.tensor.matmul_mx(out=po[:], lhsT=zc[:, m, P * g:P * g + P].bitcast(FP8X4), lhsT_scale=zs[:, m, P * g:P * g + P],
+        def mx_pass(m, n, g):
+            nc.tensor.matmul_mx(out=pos[(m, n)][:], lhsT=zc[:, m, P * g:P * g + P].bitcast(FP8X4), lhsT_scale=zs[:, m, P * g:P * g + P],
                                 rhs=wc[:, g, 512 * n:512 * n + 512].bitcast(FP8X4), rhs_scale=ws[:, g, 512 * n:512 * n + 512],
                                 start=(g == 0), stop=(g == NG - 1))
 
-        def drain(po, m, n):
+        def drain(m, n):
             ob = work.tile([P, 512], F32, name="ob%d_%d" % (m, n), tag="ob", bufs=4)
-            if O_COPY_ON_V[n]:
-                nc.vector.tensor_copy(out=ob[:], in_=po[:])
+            if n == 3:
+                nc.vector.tensor_copy(out=ob[:], in_=pos[(m, n)][:])
             else:
-                nc.scalar.copy(out=ob[:], in_=po[:])
+                nc.scalar.copy(out=ob[:], in_=pos[(m, n)][:])
             nc.sync.dma_start(out=out[m, :, 512 * n:512 * n + 512], in_=ob[:])
 
-        def xgroup(m, n):
-            po = psum.tile([P, 512], F32, name="po%d_%d" % (m, n), tag="O", bufs=2)
-            for g in range(NG):
-                mx_pass(po, m, n, g)
-            drain(po, m, n)
+        wq_slot = {}
+        for wp in range(8):
+            wq_slot[wp] = wp + 2
+        x_at = {}
+        todo = sorted((max(4 * m + 4, wq_slot[2 * n + 1] + 1), m, n) for m in range(NT - 1) for n in range(4))
+        used = 0
+        for j in range(4, 15):
+            take = 2 if len(todo) - used > 15 - j else 1
+            x_at[j] = []
+            while used < len(todo) and len(x_at[j]) < take and todo[used][0] <= j:
+                x_at[j].append((todo[used][1], todo[used][2]))
+                used += 1
+        assert used == len(todo)
 
+        setup_wb((0, 1))
         bn(0, range(H))
         stats(0)
-        prod(0)
-        wpair(0)
+        stats_s(0)
+        setup_wb((2, 3))
+        stats_b(0)
+        prod(0, 0)
+        red(0, 0)
+        heads_a(0)
+        setup_ln_gh()
+        setup_g2p(0)
+        tr_a(0)
+        heads_b(0)
+        prod(0, 1)
+        red(0, 1)
+        for t in range(4):
+            gate(0, t)
+        tr_b(0)
+        e_one(0)
+        heads_a(1)
+        heads_b(1)
+        setup_g2p(1)
         for g in range(NG):
-            red(0, g)
-        for m in range(1, NT):
-            prod(m)
-        heads(0, 0)
-        last = {}
-        for s in range(16):
-            m, g = divmod(s, 4)
-            if m + 1 < NT:
-                bn(m + 1, range(8 * g, 8 * g + 8))
-                red(m + 1, g)
-                if g == 3:
-                    stats(m + 1)
-            if s + 1 < 16:
-                heads((s + 1) // 4, (s + 1) % 4)
-            unit(m, g)
-            for wp in WP_AT.get(s, ()):
-                wpair(wp)
-            for (xm, xn) in X_AT.get(s, ()):
-                xgroup(xm, xn)
-            if m == NT - 1:
+            prod(1, g)
+
+        for j in range(0, 17):
+            m, g = divmod(j, 4)
+            for (xm, xn) in x_at.get(j, ()):
+                pos[(xm, xn)] = psum.tile([P, 512], F32, name="po%d_%d" % (xm, xn), tag="O", bufs=2)
+                for gg in range(NG):
+                    mx_pass(xm, xn, gg)
+            if j >= 13:
                 for n in range(2):
-                    if g == 0:
-                        last[n] = psum.tile([P, 512], F32, name="plast%d" % n, tag="W", bufs=2)
-                    mx_pass(last[n], m, n, g)
+                    if j == 13:
+                        pos[(3, n)] = psum.tile([P, 512], F32, name="po3_%d" % n, tag="W", bufs=3)
+                    mx_pass(3, n, j - 13)
+            if j == 15:
                 for n in range(2, 4):
-                    if g == 2:
-                        last[n] = psum.tile([P, 512], F32, name="plast%d" % n, tag="O", bufs=2)
-                        mx_pass(last[n], m, n, 0)
-                        mx_pass(last[n], m, n, 1)
-                    if g >= 2:
-                        mx_pass(last[n], m, n, g)
-        for n in range(4):
-            drain(last[n], NT - 1, n)
+                    pos[(3, n)] = psum.tile([P, 512], F32, name="po3_%d" % n, tag="O", bufs=2)
+                    for gg in range(3):
+                        mx_pass(3, n, gg)
+            if j == 16:
+                for n in range(2, 4):
+                    mx_pass(3, n, 3)
+                for n in range(4):
+                    drain(3, n)
+                break
+            add_mul(j)
+            if j < 2:
+                prod(0, j + 2)
+                red(0, j + 2)
+            late = [kk for kk in (4 * (j - 2) + 2, 4 * (j - 2) + 3) if 0 <= kk < 32]
+            now = [kk for kk in range(4 * (j - 1), 4 * j) if 0 <= kk < 32]
+            if j % 4 == 2 and m + 1 < NT:
+                stats_b(m + 1)
+            for kk in late:
+                w_copy(kk)
+            if 0 <= j - 2 < 8:
+                w_q(j - 2)
+            for (bm, lo, hi) in BN_AT.get(j, ()):
+                bn(bm, range(lo, hi))
+            if j % 4 == 1 and m + 1 < NT:
+                stats(m + 1)
+            zq(j)
+            if 4 <= j + 3 < 16:
+                red((j + 3) // 4, (j + 3) % 4)
+            nxt = j + 1 < 16
+            if nxt:
+                tr_a(j + 1)
+                tr_b(j + 1)
+                gate(j + 1, 0)
+                gate(j + 1, 1)
+            for kk in now[:2]:
+                w_tr(kk)
+            if nxt:
+                gate(j + 1, 2)
+                gate(j + 1, 3)
+            for kk in now[2:]:
+                w_tr(kk)
+            if j + 2 < 16:
+                heads_a(j + 2)
+            if j + 1 < 16:
+                e_one(j + 1)
+            for kk in now[:1]:
+                w_copy(kk)
+            if j + 2 < 16:
+                heads_b(j + 2)
+            for kk in now[1:2]:
+                w_copy(kk)
+            if j < 2:
+                setup_g2p(j + 2)
+            for (xm, xn) in x_at.get(j, ()):
+                drain(xm, xn)
+            if j % 4 == 1 and m + 1 < NT:
+                stats_s(m + 1)
+            if j < 8:
+                prod(2 + j // 4, j % 4)

@@ -29,7 +29,7 @@ FLOPS = 2 * 512 * 2048 * 2048 + 2 * 512 * 256 * 2048
 
 LD_BUFS = 22
 PINNED = True
-PROD_ON_G = (False, True, True, True)
+PROD_ON_G = (True, True, True, True)
 BN_AT = {0: ((1, 0, 16),), 1: ((1, 16, 32),), 2: ((2, 0, 8),), 3: ((2, 8, 16),), 4: ((2, 16, 24),), 5: ((2, 24, 32),),
          6: ((3, 0, 8),), 7: ((3, 8, 16),), 8: ((3, 16, 24),), 9: ((3, 24, 32),)}
 
@@ -73,31 +73,29 @@ def tile_full_tmix_params_pc_kernel(tc, y, r, k, v, g_hid, g2, r_k, ln_g, ln_b, 
             rt[m] = load(r[m], "r%d" % m)
             kt[m] = load(k[m], "k%d" % m)
 
-        yt[0] = load(y[0], "y0")
-        load_rk(0)
-        nc.sync.dma_start(out=wrow[0:1, :], in_=r_k.rearrange("(o h) i -> o (h i)", o=1))
-        nc.sync.dma_start(out=ghraw[:].rearrange("t (b d) -> t b d", b=NT), in_=g_hid.rearrange("b t d -> t b d"))
-        nc.sync.dma_start(out=lnraw[0:8, :], in_=ln_g.rearrange("(a b) -> a b", b=2 * P))
-        nc.sync.dma_start(out=lnrawb[0:8, :], in_=ln_b.rearrange("(a b) -> a b", b=2 * P))
-        g2raw = (load(g2v[0], "g2r0"), load(g2v[1], "g2r1"))
-        vt[0] = load(v[0], "v0")
-        load_rk(1)
-        yt[1] = load(y[1], "y1")
+        def small_loads():
+            nc.sync.dma_start(out=wrow[0:1, :], in_=r_k.rearrange("(o h) i -> o (h i)", o=1))
+            nc.sync.dma_start(out=ghraw[:].rearrange("t (b d) -> t b d", b=NT), in_=g_hid.rearrange("b t d -> t b d"))
+            nc.sync.dma_start(out=lnraw[0:8, :], in_=ln_g.rearrange("(a b) -> a b", b=2 * P))
+            nc.sync.dma_start(out=lnrawb[0:8, :], in_=ln_b.rearrange("(a b) -> a b", b=2 * P))
+
         load_w(0)
+        yt[0] = load(y[0], "y0")
+        small_loads()
         load_w(1)
-        vt[1] = load(v[1], "v1")
+        load_rk(0)
         load_w(2)
         load_w(3)
-        load_rk(2)
-        yt[2] = load(y[2], "y2")
+        g2raw = (load(g2v[0], "g2r0"), load(g2v[1], "g2r1"))
         load_w(4)
+        vt[0] = load(v[0], "v0")
         load_w(5)
-        vt[2] = load(v[2], "v2")
-        load_rk(3)
-        yt[3] = load(y[3], "y3")
         load_w(6)
         load_w(7)
-        vt[3] = load(v[3], "v3")
+        for m in range(1, NT):
+            load_rk(m)
+            yt[m] = load(y[m], "y%d" % m)
+            vt[m] = load(v[m], "v%d" % m)
 
         wb = const.tile([P, C], BF16, name="wb")
         lnw = const.tile([P, 16], F32, name="lnw")
@@ -111,7 +109,7 @@ def tile_full_tmix_params_pc_kernel(tc, y, r, k, v, g_hid, g2, r_k, ln_g, ln_b, 
 
         def setup_wb(js):
             for j in js:
-                pw = psum.tile([P, 512], F32, name="pwb%d" % j, tag=("W" if j < 2 else "O"), bufs=(3 if j < 2 else 2))
+                pw = psum.tile([P, 512], F32, name="pwb%d" % j, tag="X", bufs=5)
                 nc.tensor.matmul(pw[:], lhsT=ones[:], rhs=wrow[:, 512 * j:512 * j + 512], start=True, stop=True)
                 nc.scalar.copy(out=wb[:, 512 * j:512 * j + 512], in_=pw[:])
 
@@ -128,8 +126,9 @@ def tile_full_tmix_params_pc_kernel(tc, y, r, k, v, g_hid, g2, r_k, ln_g, ln_b, 
 
         def setup_g2p(g):
             for e in range(2):
-                nc.scalar.copy(out=g2p[:, e, 512 * g:512 * g + 512].rearrange("q (a f p) -> q a f p", a=2, f=2),
-                               in_=g2raw[e][:, 512 * g:512 * g + 512].rearrange("q (a p f) -> q a f p", a=2, f=2))
+                nc.gpsimd.tensor_scalar(out=g2p[:, e, 512 * g:512 * g + 512].rearrange("q (a f p) -> q a f p", a=2, f=2),
+                                        in0=g2raw[e][:, 512 * g:512 * g + 512].rearrange("q (a p f) -> q a f p", a=2, f=2),
+                                        scalar1=1.0, scalar2=0.0, op0=MUL, op1=ADD)
 
         prs, vvs, sds = {}, {}, {}
         ab, dd, rks, sts, s1s, s2s, pas, pbs, pgs, e1s, zgs, wgs, pws, pos = {}, {}, {}, {}, {}, {}, {}, {}, {}, {}, {}, {}, {}, {}
@@ -239,7 +238,7 @@ def tile_full_tmix_params_pc_kernel(tc, y, r, k, v, g_hid, g2, r_k, ln_g, ln_b, 
 
         def w_tr(kk):
             wp, g = divmod(kk, 4)
-            pws[kk] = psum.tile([P, 2, 256], F32, name="pw%d" % kk, tag="W", bufs=3)
+            pws[kk] = psum.tile([P, 2, 256], F32, name="pw%d" % kk, tag="X", bufs=5)
             for u in range(2):
                 for b2 in range(2):
                     col = 256 * g + 128 * u
@@ -273,113 +272,86 @@ def tile_full_tmix_params_pc_kernel(tc, y, r, k, v, g_hid, g2, r_k, ln_g, ln_b, 
                 nc.scalar.copy(out=ob[:], in_=pos[(m, n)][:])
             nc.sync.dma_start(out=out[m, :, 512 * n:512 * n + 512], in_=ob[:])
 
-        wq_slot = {}
-        for wp in range(8):
-            wq_slot[wp] = wp + 2
-        x_at = {}
-        todo = sorted((max(4 * m + 4, wq_slot[2 * n + 1] + 1), m, n) for m in range(NT - 1) for n in range(4))
-        used = 0
-        for j in range(4, 15):
-            take = 2 if len(todo) - used > 15 - j else 1
-            x_at[j] = []
-            while used < len(todo) and len(x_at[j]) < take and todo[used][0] <= j:
-                x_at[j].append((todo[used][1], todo[used][2]))
-                used += 1
-        assert used == len(todo)
+        def v_copies(kk):
+            return kk % 4 == 3
 
-        setup_wb((0, 1))
-        bn(0, range(H))
-        stats(0)
-        stats_s(0)
-        setup_wb((2, 3))
-        stats_b(0)
-        prod(0, 0)
-        red(0, 0)
-        heads_a(0)
-        setup_ln_gh()
-        setup_g2p(0)
+        for wp in range(8):
+            for g in range(NG):
+                w_tr(4 * wp + g)
+            if wp == 0:
+                setup_wb((0, 1, 2, 3))
+                for g in range(NG):
+                    prod(0, g)
+                for g in range(NG):
+                    setup_g2p(g)
+            if wp == 1:
+                bn(0, range(H))
+                stats(0)
+            for g in range(NG):
+                w_copy(4 * wp + g)
+            if wp >= 1:
+                w_q(wp - 1)
+            if wp == 1:
+                stats_s(0)
+                setup_ln_gh()
+            if wp == 2:
+                stats_b(0)
+                heads_a(0)
+            if wp == 3:
+                heads_a(1)
+                red(0, 0)
+                red(0, 1)
+            if wp == 4:
+                red(0, 2)
+                red(0, 3)
+            if wp == 5:
+                heads_b(0)
+                heads_b(1)
         tr_a(0)
-        heads_b(0)
-        prod(0, 1)
-        red(0, 1)
+        tr_b(0)
         for t in range(4):
             gate(0, t)
-        tr_b(0)
+        w_q(7)
         e_one(0)
-        heads_a(1)
-        heads_b(1)
-        setup_g2p(1)
         for g in range(NG):
             prod(1, g)
 
         for j in range(0, 17):
             m, g = divmod(j, 4)
-            for (xm, xn) in x_at.get(j, ()):
-                pos[(xm, xn)] = psum.tile([P, 512], F32, name="po%d_%d" % (xm, xn), tag="O", bufs=2)
-                for gg in range(NG):
-                    mx_pass(xm, xn, gg)
-            if j >= 13:
-                for n in range(2):
-                    if j == 13:
-                        pos[(3, n)] = psum.tile([P, 512], F32, name="po3_%d" % n, tag="W", bufs=3)
-                    mx_pass(3, n, j - 13)
-            if j == 15:
-                for n in range(2, 4):
-                    pos[(3, n)] = psum.tile([P, 512], F32, name="po3_%d" % n, tag="O", bufs=2)
-                    for gg in range(3):
-                        mx_pass(3, n, gg)
+            if j >= 1:
+                pm, pg_ = divmod(j - 1, 4)
+                for n in range(4):
+                    if pg_ == 0:
+                        pos[(pm, n)] = psum.tile([P, 512], F32, name="po%d_%d" % (pm, n), tag="X", bufs=5)
+                    mx_pass(pm, n, pg_)
             if j == 16:
-                for n in range(2, 4):
-                    mx_pass(3, n, 3)
                 for n in range(4):
                     drain(3, n)
                 break
             add_mul(j)
-            if j < 2:
-                prod(0, j + 2)
-                red(0, j + 2)
-            late = [kk for kk in (4 * (j - 2) + 2, 4 * (j - 2) + 3) if 0 <= kk < 32]
-            now = [kk for kk in range(4 * (j - 1), 4 * j) if 0 <= kk < 32]
             if j % 4 == 2 and m + 1 < NT:
                 stats_b(m + 1)
-            for kk in late:
-                w_copy(kk)
-            if 0 <= j - 2 < 8:
-                w_q(j - 2)
             for (bm, lo, hi) in BN_AT.get(j, ()):
                 bn(bm, range(lo, hi))
             if j % 4 == 1 and m + 1 < NT:
                 stats(m + 1)
             zq(j)
-            if 4 <= j + 3 < 16:
-                red((j + 3) // 4, (j + 3) % 4)
-            nxt = j + 1 < 16
-            if nxt:
+            if 4 <= j + 2 < 16:
+                red((j + 2) // 4, (j + 2) % 4)
+            if j + 1 < 16:
                 tr_a(j + 1)
                 tr_b(j + 1)
-                gate(j + 1, 0)
-                gate(j + 1, 1)
-            for kk in now[:2]:
-                w_tr(kk)
-            if nxt:
-                gate(j + 1, 2)
-                gate(j + 1, 3)
-            for kk in now[2:]:
-                w_tr(kk)
+                for t in range(4):
+                    gate(j + 1, t)
             if j + 2 < 16:
                 heads_a(j + 2)
             if j + 1 < 16:
                 e_one(j + 1)
-            for kk in now[:1]:
-                w_copy(kk)
             if j + 2 < 16:
                 heads_b(j + 2)
-            for kk in now[1:2]:
-                w_copy(kk)
-            if j < 2:
-                setup_g2p(j + 2)
-            for (xm, xn) in x_at.get(j, ()):
-                drain(xm, xn)
+            if j >= 4 and j % 4 == 0:
+                for n in range(4):
+                    drain(m - 1, n)
             if j % 4 == 1 and m + 1 < NT:
                 stats_s(m + 1)
             if j < 8:

@@ -193,9 +193,9 @@ def tile_full_tmix_params_pc_kernel(tc, y, r, k, v, g_hid, g2, r_k, ln_g, ln_b, 
             for hh in range(8):
                 h = 8 * g + hh
                 u, hq = divmod(hh, 4)
-                nc.scalar.activation(out=s2s[j][:, 2 * u:2 * u + 2, 32 * hq:32 * hq + 32],
-                                     in_=vt[m][:, HS * h:HS * h + HS].rearrange("t (p e) -> t e p", e=2),
-                                     func=COPY, scale=dd[m][:, h:h + 1])
+                nc.vector.tensor_scalar(out=s2s[j][:, 2 * u:2 * u + 2, 32 * hq:32 * hq + 32],
+                                        in0=vt[m][:, HS * h:HS * h + HS].rearrange("t (p e) -> t e p", e=2),
+                                        scalar1=dd[m][:, h:h + 1], scalar2=None, op0=MUL)
 
         def tr_a(j):
             pas[j] = psum.tile([P, 4, P], F32, name="pa%d" % j, tag="A", bufs=1)

@@ -29,7 +29,7 @@ FLOPS = 2 * 512 * 2048 * 2048 + 2 * 512 * 256 * 2048
 
 LD_BUFS = 22
 PINNED = True
-PROD_ON_G = (True, True, True, True)
+PROD_ON_G = (False, False, False, False)
 BN_AT = {0: ((1, 0, 16),), 1: ((1, 16, 32),), 2: ((2, 0, 8),), 3: ((2, 8, 16),), 4: ((2, 16, 24),), 5: ((2, 24, 32),),
          6: ((3, 0, 8),), 7: ((3, 8, 16),), 8: ((3, 16, 24),), 9: ((3, 24, 32),)}
 
@@ -79,22 +79,25 @@ def tile_full_tmix_params_pc_kernel(tc, y, r, k, v, g_hid, g2, r_k, ln_g, ln_b, 
             nc.sync.dma_start(out=lnraw[0:8, :], in_=ln_g.rearrange("(a b) -> a b", b=2 * P))
             nc.sync.dma_start(out=lnrawb[0:8, :], in_=ln_b.rearrange("(a b) -> a b", b=2 * P))
 
-        load_w(0)
         yt[0] = load(y[0], "y0")
         small_loads()
-        load_w(1)
+        load_w(0)
         load_rk(0)
+        load_w(1)
         load_w(2)
-        load_w(3)
         g2raw = (load(g2v[0], "g2r0"), load(g2v[1], "g2r1"))
-        load_w(4)
+        load_w(3)
         vt[0] = load(v[0], "v0")
+        load_w(4)
         load_w(5)
+        load_rk(1)
         load_w(6)
+        yt[1] = load(y[1], "y1")
         load_w(7)
-        for m in range(1, NT):
-            load_rk(m)
+        vt[1] = load(v[1], "v1")
+        for m in range(2, NT):
             yt[m] = load(y[m], "y%d" % m)
+            load_rk(m)
             vt[m] = load(v[m], "v%d" % m)
 
         wb = const.tile([P, C], BF16, name="wb")
@@ -109,7 +112,7 @@ def tile_full_tmix_params_pc_kernel(tc, y, r, k, v, g_hid, g2, r_k, ln_g, ln_b, 
 
         def setup_wb(js):
             for j in js:
-                pw = psum.tile([P, 512], F32, name="pwb%d" % j, tag="X", bufs=5)
+                pw = psum.tile([P, 512], F32, name="pwb%d" % j, tag=("A", "B", "G", "X")[j], bufs=(1, 1, 1, 5)[j])
                 nc.tensor.matmul(pw[:], lhsT=ones[:], rhs=wrow[:, 512 * j:512 * j + 512], start=True, stop=True)
                 nc.scalar.copy(out=wb[:, 512 * j:512 * j + 512], in_=pw[:])
 
@@ -126,9 +129,8 @@ def tile_full_tmix_params_pc_kernel(tc, y, r, k, v, g_hid, g2, r_k, ln_g, ln_b, 
 
         def setup_g2p(g):
             for e in range(2):
-                nc.gpsimd.tensor_scalar(out=g2p[:, e, 512 * g:512 * g + 512].rearrange("q (a f p) -> q a f p", a=2, f=2),
-                                        in0=g2raw[e][:, 512 * g:512 * g + 512].rearrange("q (a p f) -> q a f p", a=2, f=2),
-                                        scalar1=1.0, scalar2=0.0, op0=MUL, op1=ADD)
+                nc.scalar.copy(out=g2p[:, e, 512 * g:512 * g + 512].rearrange("q (a f p) -> q a f p", a=2, f=2),
+                               in_=g2raw[e][:, 512 * g:512 * g + 512].rearrange("q (a p f) -> q a f p", a=2, f=2))
 
         prs, vvs, sds = {}, {}, {}
         ab, dd, rks, sts, s1s, s2s, pas, pbs, pgs, e1s, zgs, wgs, pws, pos = {}, {}, {}, {}, {}, {}, {}, {}, {}, {}, {}, {}, {}, {}
@@ -170,7 +172,10 @@ def tile_full_tmix_params_pc_kernel(tc, y, r, k, v, g_hid, g2, r_k, ln_g, ln_b, 
                 dd[m] = work.tile([P, H], F32, name="dd%d" % m, tag="dd")
             cs = slice(512 * g, 512 * g + 512)
             eng.tensor_tensor(out=rks[m][:, cs], in0=rt[m][:, cs], in1=kt[m][:, cs], op=MUL)
-            eng.tensor_tensor(out=rks[m][:, cs], in0=rks[m][:, cs], in1=wb[:, cs], op=MUL)
+
+        def prod_b(m, g):
+            cs = slice(512 * g, 512 * g + 512)
+            nc.vector.tensor_tensor(out=rks[m][:, cs], in0=rks[m][:, cs], in1=wb[:, cs], op=MUL)
 
         def red(m, g):
             nc.vector.tensor_reduce(out=dd[m][:, 8 * g:8 * g + 8],
@@ -193,9 +198,9 @@ def tile_full_tmix_params_pc_kernel(tc, y, r, k, v, g_hid, g2, r_k, ln_g, ln_b, 
             for hh in range(8):
                 h = 8 * g + hh
                 u, hq = divmod(hh, 4)
-                nc.vector.tensor_scalar(out=s2s[j][:, 2 * u:2 * u + 2, 32 * hq:32 * hq + 32],
-                                        in0=vt[m][:, HS * h:HS * h + HS].rearrange("t (p e) -> t e p", e=2),
-                                        scalar1=dd[m][:, h:h + 1], scalar2=None, op0=MUL)
+                nc.scalar.activation(out=s2s[j][:, 2 * u:2 * u + 2, 32 * hq:32 * hq + 32],
+                                     in_=vt[m][:, HS * h:HS * h + HS].rearrange("t (p e) -> t e p", e=2),
+                                     func=COPY, scale=dd[m][:, h:h + 1])
 
         def tr_a(j):
             pas[j] = psum.tile([P, 4, P], F32, name="pa%d" % j, tag="A", bufs=1)
@@ -225,8 +230,10 @@ def tile_full_tmix_params_pc_kernel(tc, y, r, k, v, g_hid, g2, r_k, ln_g, ln_b, 
                 nc.scalar.activation(out=e1s[j][:, t, :], in_=pas[j][:, t, :], func=IDENT,
                                      bias=lnT[:, 16 + blk:17 + blk], scale=lnT[:, blk:blk + 1])
 
-        def add_mul(j):
+        def add_(j):
             nc.vector.tensor_tensor(out=e1s[j][:], in0=e1s[j][:], in1=pbs[j][:], op=ADD)
+
+        def mul_(j):
             zgs[j] = work.tile([P, P, 4], BF16, name="zg%d" % j, tag="zg", bufs=3, align_bytes=64)
             nc.vector.tensor_tensor(out=zgs[j][:], in0=e1s[j][:].rearrange("p t r -> p r t"),
                                     in1=pgs[j][:].rearrange("p t r -> p r t"), op=MUL)
@@ -249,10 +256,7 @@ def tile_full_tmix_params_pc_kernel(tc, y, r, k, v, g_hid, g2, r_k, ln_g, ln_b, 
             if g == 0:
                 wgs[wp] = work.tile([P, 4096], BF16, name="wg%d" % wp, tag="wg", bufs=2, align_bytes=64)
             dst = wgs[wp][:].bitcast(F32).rearrange("p (g c u) -> p g c u", g=NG, u=2)[:, g, :, :]
-            if kk % 4 == 3:
-                nc.vector.tensor_copy(out=dst, in_=pws[kk][:].rearrange("p u c -> p c u"))
-            else:
-                nc.scalar.copy(out=dst, in_=pws[kk][:].rearrange("p u c -> p c u"))
+            nc.scalar.copy(out=dst, in_=pws[kk][:].rearrange("p u c -> p c u"))
 
         def w_q(wp):
             for g in range(NG):
@@ -275,46 +279,64 @@ def tile_full_tmix_params_pc_kernel(tc, y, r, k, v, g_hid, g2, r_k, ln_g, ln_b, 
         def v_copies(kk):
             return kk % 4 == 3
 
+        def dot2(m, g):
+            prod(m, g)
+            prod(m, g + 1)
+            prod_b(m, g)
+            prod_b(m, g + 1)
+            red(m, g)
+            red(m, g + 1)
+
+        setup_wb((0, 1, 2, 3))
+        bn(0, range(H))
+        stats(0)
+        stats_s(0)
+        stats_b(0)
         for wp in range(8):
             for g in range(NG):
                 w_tr(4 * wp + g)
-            if wp == 0:
-                setup_wb((0, 1, 2, 3))
-                for g in range(NG):
-                    prod(0, g)
-                for g in range(NG):
-                    setup_g2p(g)
             if wp == 1:
-                bn(0, range(H))
-                stats(0)
+                setup_ln_gh()
             for g in range(NG):
                 w_copy(4 * wp + g)
             if wp >= 1:
                 w_q(wp - 1)
-            if wp == 1:
-                stats_s(0)
-                setup_ln_gh()
-            if wp == 2:
-                stats_b(0)
+            if wp == 0:
                 heads_a(0)
-            if wp == 3:
                 heads_a(1)
-                red(0, 0)
-                red(0, 1)
-            if wp == 4:
-                red(0, 2)
-                red(0, 3)
-            if wp == 5:
+            if wp in (0, 1):
+                dot2(0, 2 * wp)
+            if wp == 2:
+                setup_g2p(0)
+                setup_g2p(1)
+            if wp == 3:
                 heads_b(0)
                 heads_b(1)
+            if wp == 4:
+                setup_g2p(2)
+                setup_g2p(3)
+            if wp in (5, 6):
+                dot2(1, 2 * wp - 10)
+            if wp == 7:
+                bn(1, range(H))
+                stats(1)
         tr_a(0)
         tr_b(0)
         for t in range(4):
             gate(0, t)
         w_q(7)
         e_one(0)
-        for g in range(NG):
-            prod(1, g)
+        stats_s(1)
+
+        fill = {}
+        for m in (2, 3):
+            s0 = 1 + 6 * (m - 2)
+            fill[s0] = [("bn", m, 0), ("bn", m, 1)]
+            fill[s0 + 1] = [("bn", m, 2), ("bn", m, 3)]
+            fill[s0 + 2] = [("sa", m, 0), ("pr", m, 0)]
+            fill[s0 + 3] = [("sb", m, 0), ("pr", m, 1)]
+            fill[s0 + 4] = [("pr", m, 2)]
+            fill[s0 + 5] = [("pr", m, 3)]
 
         for j in range(0, 17):
             m, g = divmod(j, 4)
@@ -328,16 +350,29 @@ def tile_full_tmix_params_pc_kernel(tc, y, r, k, v, g_hid, g2, r_k, ln_g, ln_b, 
                 for n in range(4):
                     drain(3, n)
                 break
-            add_mul(j)
-            if j % 4 == 2 and m + 1 < NT:
-                stats_b(m + 1)
-            for (bm, lo, hi) in BN_AT.get(j, ()):
-                bn(bm, range(lo, hi))
-            if j % 4 == 1 and m + 1 < NT:
-                stats(m + 1)
+            todo = fill.get(j, ())
+            add_(j)
+            if j == 0:
+                stats_b(1)
+            for (kind, fm, part) in todo:
+                if kind == "sb":
+                    stats_b(fm)
+                if kind == "bn" and part % 2 == 0:
+                    bn(fm, range(8 * part, 8 * part + 8))
+                if kind == "pr":
+                    prod(fm, part)
+            mul_(j)
+            for (kind, fm, part) in todo:
+                if kind == "bn" and part % 2 == 1:
+                    bn(fm, range(8 * part, 8 * part + 8))
+                if kind == "sa":
+                    stats(fm)
+                if kind == "pr":
+                    prod_b(fm, part)
             zq(j)
-            if 4 <= j + 2 < 16:
-                red((j + 2) // 4, (j + 2) % 4)
+            for (kind, fm, part) in todo:
+                if kind == "pr":
+                    red(fm, part)
             if j + 1 < 16:
                 tr_a(j + 1)
                 tr_b(j + 1)
@@ -352,7 +387,6 @@ def tile_full_tmix_params_pc_kernel(tc, y, r, k, v, g_hid, g2, r_k, ln_g, ln_b, 
             if j >= 4 and j % 4 == 0:
                 for n in range(4):
                     drain(m - 1, n)
-            if j % 4 == 1 and m + 1 < NT:
-                stats_s(m + 1)
-            if j < 8:
-                prod(2 + j // 4, j % 4)
+            for (kind, fm, part) in todo:
+                if kind == "sa":
+                    stats_s(fm)

@@ -28,6 +28,8 @@ EPS = 0.00064
 FLOPS = 2 * 512 * 2048 * 2048 + 2 * 512 * 256 * 2048
 
 LD_BUFS = 22
+HB_ON_V = 16
+HA_ON_V = 16
 PINNED = True
 PROD_ON_G = (False, False, False, False)
 BN_AT = {0: ((1, 0, 16),), 1: ((1, 16, 32),), 2: ((2, 0, 8),), 3: ((2, 8, 16),), 4: ((2, 16, 24),), 5: ((2, 24, 32),),
@@ -85,7 +87,9 @@ def tile_full_tmix_params_pc_kernel(tc, y, r, k, v, g_hid, g2, r_k, ln_g, ln_b, 
         load_rk(0)
         load_w(1)
         load_w(2)
-        g2raw = (load(g2v[0], "g2r0"), load(g2v[1], "g2r1"))
+        g2s = const.tile([P, 2, C], BF16, name="g2s")
+        for e in range(2):
+            nc.sync.dma_start(out=g2s[:, e, :], in_=g2v[e])
         load_w(3)
         vt[0] = load(v[0], "v0")
         load_w(4)
@@ -104,7 +108,6 @@ def tile_full_tmix_params_pc_kernel(tc, y, r, k, v, g_hid, g2, r_k, ln_g, ln_b, 
         lnw = const.tile([P, 16], F32, name="lnw")
         lnT = const.tile([P, 32], F32, name="lnT")
         ghT = const.tile([P, 2, 512], BF16, name="ghT")
-        g2p = const.tile([P, 2, C], BF16, name="g2p")
         wc = const.tile([P, NG, CO], U32, name="wc", align_bytes=64)
         ws = const.tile([P, NG, CO], U8, name="ws", align_bytes=64)
         zc = const.tile([P, NT, 512], U32, name="zc", align_bytes=64)
@@ -126,11 +129,6 @@ def tile_full_tmix_params_pc_kernel(tc, y, r, k, v, g_hid, g2, r_k, ln_g, ln_b, 
             for m in range(NT):
                 nc.tensor.transpose(pg[:, P * m:P * m + P], ghraw[:].bitcast(F32)[:, P * m:P * m + P], ident[:])
             nc.vector.tensor_copy(out=ghT[:], in_=pg[:].bitcast(BF16).rearrange("q (n e) -> q e n", e=2))
-
-        def setup_g2p(g):
-            for e in range(2):
-                nc.scalar.copy(out=g2p[:, e, 512 * g:512 * g + 512].rearrange("q (a f p) -> q a f p", a=2, f=2),
-                               in_=g2raw[e][:, 512 * g:512 * g + 512].rearrange("q (a p f) -> q a f p", a=2, f=2))
 
         prs, vvs, sds = {}, {}, {}
         ab, dd, rks, sts, s1s, s2s, pas, pbs, pgs, e1s, zgs, wgs, pws, pos = {}, {}, {}, {}, {}, {}, {}, {}, {}, {}, {}, {}, {}, {}
@@ -188,9 +186,14 @@ def tile_full_tmix_params_pc_kernel(tc, y, r, k, v, g_hid, g2, r_k, ln_g, ln_b, 
             for hh in range(8):
                 h = 8 * g + hh
                 u, hq = divmod(hh, 4)
-                nc.scalar.activation(out=s1s[j][:, 2 * u:2 * u + 2, 32 * hq:32 * hq + 32],
-                                     in_=yt[m][:, HS * h:HS * h + HS].rearrange("t (p e) -> t e p", e=2),
-                                     func=IDENT, bias=ab[m][:, 1, h:h + 1], scale=ab[m][:, 0, h:h + 1])
+                if j >= HA_ON_V:
+                    nc.vector.tensor_scalar(out=s1s[j][:, 2 * u:2 * u + 2, 32 * hq:32 * hq + 32],
+                                            in0=yt[m][:, HS * h:HS * h + HS].rearrange("t (p e) -> t e p", e=2),
+                                            scalar1=ab[m][:, 0, h:h + 1], scalar2=ab[m][:, 1, h:h + 1], op0=MUL, op1=ADD)
+                else:
+                    nc.scalar.activation(out=s1s[j][:, 2 * u:2 * u + 2, 32 * hq:32 * hq + 32],
+                                         in_=yt[m][:, HS * h:HS * h + HS].rearrange("t (p e) -> t e p", e=2),
+                                         func=IDENT, bias=ab[m][:, 1, h:h + 1], scale=ab[m][:, 0, h:h + 1])
 
         def heads_b(j):
             m, g = divmod(j, 4)
@@ -198,9 +201,14 @@ def tile_full_tmix_params_pc_kernel(tc, y, r, k, v, g_hid, g2, r_k, ln_g, ln_b, 
             for hh in range(8):
                 h = 8 * g + hh
                 u, hq = divmod(hh, 4)
-                nc.scalar.activation(out=s2s[j][:, 2 * u:2 * u + 2, 32 * hq:32 * hq + 32],
-                                     in_=vt[m][:, HS * h:HS * h + HS].rearrange("t (p e) -> t e p", e=2),
-                                     func=COPY, scale=dd[m][:, h:h + 1])
+                if j >= HB_ON_V:
+                    nc.vector.tensor_scalar(out=s2s[j][:, 2 * u:2 * u + 2, 32 * hq:32 * hq + 32],
+                                            in0=vt[m][:, HS * h:HS * h + HS].rearrange("t (p e) -> t e p", e=2),
+                                            scalar1=dd[m][:, h:h + 1], scalar2=None, op0=MUL)
+                else:
+                    nc.scalar.activation(out=s2s[j][:, 2 * u:2 * u + 2, 32 * hq:32 * hq + 32],
+                                         in_=vt[m][:, HS * h:HS * h + HS].rearrange("t (p e) -> t e p", e=2),
+                                         func=COPY, scale=dd[m][:, h:h + 1])
 
         def tr_a(j):
             pas[j] = psum.tile([P, 4, P], F32, name="pa%d" % j, tag="A", bufs=1)
@@ -219,7 +227,8 @@ def tile_full_tmix_params_pc_kernel(tc, y, r, k, v, g_hid, g2, r_k, ln_g, ln_b, 
             if True:
                 blk = 4 * g + t
                 for e in range(2):
-                    nc.tensor.matmul(pgs[j][:, t, :], lhsT=g2p[:, e, P * blk:P * blk + P], rhs=ghT[:, e, P * m:P * m + P],
+                    cols = g2s[:, e, 256 * (blk // 2):256 * (blk // 2) + 256].rearrange("q (p f) -> q f p", f=2)[:, blk % 2, :]
+                    nc.tensor.matmul(pgs[j][:, t, :], lhsT=cols, rhs=ghT[:, e, P * m:P * m + P],
                                      start=(e == 0), stop=(e == 1))
 
         def e_one(j):
@@ -270,7 +279,7 @@ def tile_full_tmix_params_pc_kernel(tc, y, r, k, v, g_hid, g2, r_k, ln_g, ln_b, 
 
         def drain(m, n):
             ob = work.tile([P, 512], F32, name="ob%d_%d" % (m, n), tag="ob", bufs=4)
-            if n == 3:
+            if m == NT - 1 and n % 2 == 1:
                 nc.vector.tensor_copy(out=ob[:], in_=pos[(m, n)][:])
             else:
                 nc.scalar.copy(out=ob[:], in_=pos[(m, n)][:])
@@ -295,7 +304,7 @@ def tile_full_tmix_params_pc_kernel(tc, y, r, k, v, g_hid, g2, r_k, ln_g, ln_b, 
         for wp in range(8):
             for g in range(NG):
                 w_tr(4 * wp + g)
-            if wp == 1:
+            if wp == 2:
                 setup_ln_gh()
             for g in range(NG):
                 w_copy(4 * wp + g)
@@ -306,15 +315,9 @@ def tile_full_tmix_params_pc_kernel(tc, y, r, k, v, g_hid, g2, r_k, ln_g, ln_b, 
                 heads_a(1)
             if wp in (0, 1):
                 dot2(0, 2 * wp)
-            if wp == 2:
-                setup_g2p(0)
-                setup_g2p(1)
             if wp == 3:
                 heads_b(0)
                 heads_b(1)
-            if wp == 4:
-                setup_g2p(2)
-                setup_g2p(3)
             if wp in (5, 6):
                 dot2(1, 2 * wp - 10)
             if wp == 7:
@@ -328,18 +331,47 @@ def tile_full_tmix_params_pc_kernel(tc, y, r, k, v, g_hid, g2, r_k, ln_g, ln_b, 
         e_one(0)
         stats_s(1)
 
-        fill = {}
-        for m in (2, 3):
-            s0 = 1 + 6 * (m - 2)
-            fill[s0] = [("bn", m, 0), ("bn", m, 1)]
-            fill[s0 + 1] = [("bn", m, 2), ("bn", m, 3)]
-            fill[s0 + 2] = [("sa", m, 0), ("pr", m, 0)]
-            fill[s0 + 3] = [("sb", m, 0), ("pr", m, 1)]
-            fill[s0 + 4] = [("pr", m, 2)]
-            fill[s0 + 5] = [("pr", m, 3)]
+        tr_a(1)
+        e_one(1)
+        heads_a(2)
+
+        fill = {1: (("bn", 2, 0), ("bn", 2, 1)), 2: (("bn", 2, 2), ("bn", 2, 3), ("sa", 2, 0)), 3: (("pr", 2, 0),),
+                4: (("sb", 2, 0), ("pr", 2, 1)), 5: (("pr", 2, 2), ("bn", 3, 0)), 6: (("pr", 2, 3), ("bn", 3, 1)),
+                7: (("bn", 3, 2), ("bn", 3, 3), ("sa", 3, 0)), 8: (("pr", 3, 0),), 9: (("sb", 3, 0), ("pr", 3, 1)),
+                10: (("pr", 3, 2),), 11: (("pr", 3, 3),)}
 
         for j in range(0, 17):
             m, g = divmod(j, 4)
+            todo = fill.get(j, ())
+            if j < 16:
+                add_(j)
+                if j == 0:
+                    stats_b(1)
+                for (kind, fm, part) in todo:
+                    if kind == "sb":
+                        stats_b(fm)
+                    if kind == "bn" and part % 2 == 0:
+                        bn(fm, range(8 * part, 8 * part + 8))
+                    if kind == "pr":
+                        prod(fm, part)
+                mul_(j)
+                for (kind, fm, part) in todo:
+                    if kind == "bn" and part % 2 == 1:
+                        bn(fm, range(8 * part, 8 * part + 8))
+                    if kind == "sa":
+                        stats(fm)
+                    if kind == "pr":
+                        prod_b(fm, part)
+                zq(j)
+                for (kind, fm, part) in todo:
+                    if kind == "pr":
+                        red(fm, part)
+            if j + 1 < 16:
+                tr_b(j + 1)
+                for t in range(4):
+                    gate(j + 1, t)
+            if j + 2 < 16:
+                tr_a(j + 2)
             if j >= 1:
                 pm, pg_ = divmod(j - 1, 4)
                 for n in range(4):
@@ -350,43 +382,15 @@ def tile_full_tmix_params_pc_kernel(tc, y, r, k, v, g_hid, g2, r_k, ln_g, ln_b, 
                 for n in range(4):
                     drain(3, n)
                 break
-            todo = fill.get(j, ())
-            add_(j)
-            if j == 0:
-                stats_b(1)
-            for (kind, fm, part) in todo:
-                if kind == "sb":
-                    stats_b(fm)
-                if kind == "bn" and part % 2 == 0:
-                    bn(fm, range(8 * part, 8 * part + 8))
-                if kind == "pr":
-                    prod(fm, part)
-            mul_(j)
-            for (kind, fm, part) in todo:
-                if kind == "bn" and part % 2 == 1:
-                    bn(fm, range(8 * part, 8 * part + 8))
-                if kind == "sa":
-                    stats(fm)
-                if kind == "pr":
-                    prod_b(fm, part)
-            zq(j)
-            for (kind, fm, part) in todo:
-                if kind == "pr":
-                    red(fm, part)
-            if j + 1 < 16:
-                tr_a(j + 1)
-                tr_b(j + 1)
-                for t in range(4):
-                    gate(j + 1, t)
-            if j + 2 < 16:
-                heads_a(j + 2)
-            if j + 1 < 16:
-                e_one(j + 1)
-            if j + 2 < 16:
-                heads_b(j + 2)
-            if j >= 4 and j % 4 == 0:
-                for n in range(4):
-                    drain(m - 1, n)
             for (kind, fm, part) in todo:
                 if kind == "sa":
                     stats_s(fm)
+            if j + 2 < 16:
+                heads_b(j + 2)
+            if j + 2 < 16:
+                e_one(j + 2)
+            if j + 3 < 16:
+                heads_a(j + 3)
+            if j >= 4 and j % 4 == 0:
+                for n in range(4):
+                    drain(m - 1, n)

@@ -11,386 +11,325 @@ FP8X4 = mybir.dt.float8_e4m3fn_x4
 ADD = mybir.AluOpType.add
 SUB = mybir.AluOpType.subtract
 MUL = mybir.AluOpType.mult
-IDENT = mybir.ActivationFunctionType.Identity
+IDENTITY = mybir.ActivationFunctionType.Identity
 COPY = mybir.ActivationFunctionType.Copy
 SQRT = mybir.ActivationFunctionType.Sqrt
-AX_X = mybir.AxisListType.X
+AXIS_X = mybir.AxisListType.X
 
 P = 128
-NT = 4
+TILES = 4
 C = 2048
 CO = 2048
-HS = 64
-H = C // HS
-NG = 4
+HEAD = 64
+HEADS = C // HEAD
+PASSES = 4
+UNITS = TILES * PASSES
+PAIRS = 8
 EPS = 0.00064
 
 FLOPS = 2 * 512 * 2048 * 2048 + 2 * 512 * 256 * 2048
-
-LD_BUFS = 22
-HB_ON_V = 16
-HA_ON_V = 16
-PINNED = True
-PROD_ON_G = (False, False, False, False)
-BN_AT = {0: ((1, 0, 16),), 1: ((1, 16, 32),), 2: ((2, 0, 8),), 3: ((2, 8, 16),), 4: ((2, 16, 24),), 5: ((2, 24, 32),),
-         6: ((3, 0, 8),), 7: ((3, 8, 16),), 8: ((3, 16, 24),), 9: ((3, 24, 32),)}
 
 
 def tile_full_tmix_params_pc_kernel(tc, y, r, k, v, g_hid, g2, r_k, ln_g, ln_b, W_o, out):
     nc = tc.nc
     with ExitStack() as ctx:
         const = ctx.enter_context(tc.tile_pool(name="const", bufs=1))
-        ld = ctx.enter_context(tc.tile_pool(name="ld", bufs=LD_BUFS))
+        ld = ctx.enter_context(tc.tile_pool(name="ld", bufs=22))
         work = ctx.enter_context(tc.tile_pool(name="work", bufs=2))
         psum = ctx.enter_context(tc.psum_pool(name="psum", bufs=1))
-        if PINNED:
-            ctx.enter_context(tc.manual_schedule())
+        ctx.enter_context(tc.manual_schedule())
 
         ident = const.tile([P, P], F32, name="ident")
         make_identity(nc, ident[:])
-        wrow = ld.tile([P, C], BF16, name="wrow", tag="ld")
-        nc.vector.memset(wrow[:], 0.0)
-        lnraw = const.tile([P, 2 * P], BF16, name="lnraw")
-        nc.vector.memset(lnraw[:], 0.0)
-        lnrawb = const.tile([P, 2 * P], BF16, name="lnrawb")
-        nc.vector.memset(lnrawb[:], 0.0)
+        rk_row = ld.tile([P, C], BF16, name="rk_row", tag="ld")
+        nc.vector.memset(rk_row[:], 0.0)
+        lng_rows = const.tile([P, 2 * P], BF16, name="lng_rows")
+        nc.vector.memset(lng_rows[:], 0.0)
+        lnb_rows = const.tile([P, 2 * P], BF16, name="lnb_rows")
+        nc.vector.memset(lnb_rows[:], 0.0)
         ones = const.tile([P, P], BF16, name="ones")
         nc.vector.memset(ones[:], 1.0)
-        ghraw = const.tile([P, NT * 256], BF16, name="ghraw")
+        gh_rows = const.tile([P, TILES * 256], BF16, name="gh_rows")
+        g2_sb = const.tile([P, 2, C], BF16, name="g2_sb")
+
+        y_sb, r_sb, k_sb, v_sb, w_sb = {}, {}, {}, {}, {}
 
         def load(src, label):
             t = ld.tile([P, C], BF16, name=label, tag="ld")
             nc.sync.dma_start(out=t[:], in_=src)
             return t
 
-        yt, rt, kt, vt, wr = {}, {}, {}, {}, {}
-        g2v = g2.rearrange("(q e) c -> e q c", e=2)
-
-        def load_w(wp):
-            for b2 in range(2):
-                row = 256 * wp + 128 * b2
-                wr[(wp, b2)] = load(W_o[row:row + 128, :], "w%d_%d" % (wp, b2))
+        def load_y(m):
+            y_sb[m] = load(y[m], "y%d" % m)
 
         def load_rk(m):
-            rt[m] = load(r[m], "r%d" % m)
-            kt[m] = load(k[m], "k%d" % m)
+            r_sb[m] = load(r[m], "r%d" % m)
+            k_sb[m] = load(k[m], "k%d" % m)
 
-        def small_loads():
-            nc.sync.dma_start(out=wrow[0:1, :], in_=r_k.rearrange("(o h) i -> o (h i)", o=1))
-            nc.sync.dma_start(out=ghraw[:].rearrange("t (b d) -> t b d", b=NT), in_=g_hid.rearrange("b t d -> t b d"))
-            nc.sync.dma_start(out=lnraw[0:8, :], in_=ln_g.rearrange("(a b) -> a b", b=2 * P))
-            nc.sync.dma_start(out=lnrawb[0:8, :], in_=ln_b.rearrange("(a b) -> a b", b=2 * P))
+        def load_v(m):
+            v_sb[m] = load(v[m], "v%d" % m)
 
-        yt[0] = load(y[0], "y0")
-        small_loads()
+        def load_w(pair):
+            for b in range(2):
+                row = 256 * pair + P * b
+                w_sb[(pair, b)] = load(W_o[row:row + P, :], "w%d_%d" % (pair, b))
+
+        load_y(0)
+        nc.sync.dma_start(out=rk_row[0:1, :], in_=r_k.rearrange("(o h) i -> o (h i)", o=1))
+        nc.sync.dma_start(out=gh_rows[:].rearrange("t (b d) -> t b d", b=TILES), in_=g_hid.rearrange("b t d -> t b d"))
+        nc.sync.dma_start(out=lng_rows[0:8, :], in_=ln_g.rearrange("(a b) -> a b", b=2 * P))
+        nc.sync.dma_start(out=lnb_rows[0:8, :], in_=ln_b.rearrange("(a b) -> a b", b=2 * P))
         load_w(0)
         load_rk(0)
         load_w(1)
         load_w(2)
-        g2s = const.tile([P, 2, C], BF16, name="g2s")
-        for e in range(2):
-            nc.sync.dma_start(out=g2s[:, e, :], in_=g2v[e])
         load_w(3)
-        vt[0] = load(v[0], "v0")
+        load_y(1)
         load_w(4)
         load_w(5)
         load_rk(1)
+        load_v(0)
         load_w(6)
-        yt[1] = load(y[1], "y1")
+        for e in range(2):
+            nc.sync.dma_start(out=g2_sb[:, e, :], in_=g2.rearrange("(q e) c -> e q c", e=2)[e])
         load_w(7)
-        vt[1] = load(v[1], "v1")
-        for m in range(2, NT):
-            yt[m] = load(y[m], "y%d" % m)
-            load_rk(m)
-            vt[m] = load(v[m], "v%d" % m)
+        load_y(2)
+        load_v(1)
+        load_rk(2)
+        load_y(3)
+        load_v(2)
+        load_rk(3)
+        load_v(3)
 
-        wb = const.tile([P, C], BF16, name="wb")
-        lnw = const.tile([P, 16], F32, name="lnw")
-        lnT = const.tile([P, 32], F32, name="lnT")
-        ghT = const.tile([P, 2, 512], BF16, name="ghT")
-        wc = const.tile([P, NG, CO], U32, name="wc", align_bytes=64)
-        ws = const.tile([P, NG, CO], U8, name="ws", align_bytes=64)
-        zc = const.tile([P, NT, 512], U32, name="zc", align_bytes=64)
-        zs = const.tile([P, NT, 512], U8, name="zs", align_bytes=64)
+        rk_all = const.tile([P, C], BF16, name="rk_all")
+        ln_words = const.tile([P, 16], F32, name="ln_words")
+        ln_cols = const.tile([P, 32], F32, name="ln_cols")
+        gh_t = const.tile([P, 2, 512], BF16, name="gh_t")
+        w_codes = const.tile([P, PASSES, CO], U32, name="w_codes", align_bytes=64)
+        w_scales = const.tile([P, PASSES, CO], U8, name="w_scales", align_bytes=64)
+        z_codes = const.tile([P, TILES, 512], U32, name="z_codes", align_bytes=64)
+        z_scales = const.tile([P, TILES, 512], U8, name="z_scales", align_bytes=64)
 
-        def setup_wb(js):
-            for j in js:
-                pw = psum.tile([P, 512], F32, name="pwb%d" % j, tag=("A", "B", "G", "X")[j], bufs=(1, 1, 1, 5)[j])
-                nc.tensor.matmul(pw[:], lhsT=ones[:], rhs=wrow[:, 512 * j:512 * j + 512], start=True, stop=True)
-                nc.scalar.copy(out=wb[:, 512 * j:512 * j + 512], in_=pw[:])
+        def spread_r_k():
+            for j in range(4):
+                acc = psum.tile([P, 512], F32, name="rk_ps%d" % j, tag=("A", "B", "G", "X")[j], bufs=(1, 1, 1, 5)[j])
+                nc.tensor.matmul(acc[:], lhsT=ones[:], rhs=rk_row[:, 512 * j:512 * j + 512], start=True, stop=True)
+                nc.scalar.copy(out=rk_all[:, 512 * j:512 * j + 512], in_=acc[:])
 
-        def setup_ln_gh():
-            pl = psum.tile([P, 2, P], F32, name="pl", tag="B", bufs=1)
-            nc.tensor.transpose(pl[:, 0, :], lnraw[:].bitcast(F32), ident[:])
-            nc.tensor.transpose(pl[:, 1, :], lnrawb[:].bitcast(F32), ident[:])
-            nc.vector.tensor_copy(out=lnw[:].rearrange("p (a b) -> p a b", a=2), in_=pl[:, :, 0:8])
-            nc.vector.tensor_copy(out=lnT[:], in_=lnw[:].bitcast(BF16))
-            pg = psum.tile([P, 512], F32, name="pg", tag="G", bufs=1)
-            for m in range(NT):
-                nc.tensor.transpose(pg[:, P * m:P * m + P], ghraw[:].bitcast(F32)[:, P * m:P * m + P], ident[:])
-            nc.vector.tensor_copy(out=ghT[:], in_=pg[:].bitcast(BF16).rearrange("q (n e) -> q e n", e=2))
+        def turn_ln_and_g_hid():
+            ln_ps = psum.tile([P, 2, P], F32, name="ln_ps", tag="B", bufs=1)
+            nc.tensor.transpose(ln_ps[:, 0, :], lng_rows[:].bitcast(F32), ident[:])
+            nc.tensor.transpose(ln_ps[:, 1, :], lnb_rows[:].bitcast(F32), ident[:])
+            nc.vector.tensor_copy(out=ln_words[:].rearrange("p (a b) -> p a b", a=2), in_=ln_ps[:, :, 0:8])
+            nc.vector.tensor_copy(out=ln_cols[:], in_=ln_words[:].bitcast(BF16))
+            gh_ps = psum.tile([P, 512], F32, name="gh_ps", tag="G", bufs=1)
+            for m in range(TILES):
+                nc.tensor.transpose(gh_ps[:, P * m:P * m + P], gh_rows[:].bitcast(F32)[:, P * m:P * m + P], ident[:])
+            nc.vector.tensor_copy(out=gh_t[:], in_=gh_ps[:].bitcast(BF16).rearrange("q (n e) -> q e n", e=2))
 
-        prs, vvs, sds = {}, {}, {}
-        ab, dd, rks, sts, s1s, s2s, pas, pbs, pgs, e1s, zgs, wgs, pws, pos = {}, {}, {}, {}, {}, {}, {}, {}, {}, {}, {}, {}, {}, {}
+        bn_out, sums, var_eps, std, a_b, dots, rkw = {}, {}, {}, {}, {}, {}, {}
+        s1, s2, s1_ps, s2_ps, gate_ps, e1, z_bf, w_bf, w_ps, out_ps = {}, {}, {}, {}, {}, {}, {}, {}, {}, {}
 
-        def bn(m, heads):
-            if m not in sts:
-                sts[m] = work.tile([P, H, 6], F32, name="st%d" % m, tag="st")
-            for h in heads:
-                nc.vector.bn_stats(out=sts[m][:, h, :], in_=yt[m][:, HS * h:HS * h + HS])
+        def bn_part(m, part):
+            if part == 0:
+                bn_out[m] = work.tile([P, HEADS, 6], F32, name="bn%d" % m, tag="bn")
+            for h in range(8 * part, 8 * part + 8):
+                nc.vector.bn_stats(out=bn_out[m][:, h, :], in_=y_sb[m][:, HEAD * h:HEAD * h + HEAD])
 
-        def stats(m):
-            st = sts[m]
-            pr = work.tile([P, H, 2], F32, name="pr%d" % m, tag="pr")
-            nc.vector.tensor_tensor(out=pr[:], in0=st[:, :, 1:3], in1=st[:, :, 4:6], op=ADD)
-            dm = work.tile([P, H], F32, name="dm%d" % m, tag="dm")
-            nc.vector.tensor_tensor(out=dm[:], in0=st[:, :, 1], in1=st[:, :, 4], op=SUB)
-            qe = work.tile([P, H], F32, name="qe%d" % m, tag="qe")
-            nc.vector.tensor_scalar(out=qe[:], in0=pr[:, :, 1], scalar1=1.0 / HS, scalar2=EPS, op0=MUL, op1=ADD)
-            d2 = work.tile([P, H], F32, name="d2%d" % m, tag="d2")
-            nc.vector.tensor_tensor(out=d2[:], in0=dm[:], in1=dm[:], op=MUL)
-            vv = work.tile([P, H], F32, name="vv%d" % m, tag="vv")
-            nc.vector.scalar_tensor_tensor(out=vv[:], in0=d2[:], scalar=0.25, in1=qe[:], op0=MUL, op1=ADD)
-            prs[m] = pr
-            vvs[m] = vv
+        def variance(m):
+            st = bn_out[m]
+            sums[m] = work.tile([P, HEADS, 2], F32, name="sums%d" % m, tag="sums")
+            nc.vector.tensor_tensor(out=sums[m][:], in0=st[:, :, 1:3], in1=st[:, :, 4:6], op=ADD)
+            diff = work.tile([P, HEADS], F32, name="diff%d" % m, tag="diff")
+            nc.vector.tensor_tensor(out=diff[:], in0=st[:, :, 1], in1=st[:, :, 4], op=SUB)
+            within = work.tile([P, HEADS], F32, name="within%d" % m, tag="within")
+            nc.vector.tensor_scalar(out=within[:], in0=sums[m][:, :, 1], scalar1=1.0 / HEAD, scalar2=EPS, op0=MUL, op1=ADD)
+            diff2 = work.tile([P, HEADS], F32, name="diffsq%d" % m, tag="diffsq")
+            nc.vector.tensor_tensor(out=diff2[:], in0=diff[:], in1=diff[:], op=MUL)
+            var_eps[m] = work.tile([P, HEADS], F32, name="vareps%d" % m, tag="vareps")
+            nc.vector.scalar_tensor_tensor(out=var_eps[m][:], in0=diff2[:], scalar=0.25, in1=within[:], op0=MUL, op1=ADD)
 
-        def stats_s(m):
-            sds[m] = work.tile([P, H], F32, name="sd%d" % m, tag="sd")
-            nc.scalar.activation(out=sds[m][:], in_=vvs[m][:], func=SQRT)
+        def root(m):
+            std[m] = work.tile([P, HEADS], F32, name="std%d" % m, tag="std")
+            nc.scalar.activation(out=std[m][:], in_=var_eps[m][:], func=SQRT)
 
-        def stats_b(m):
-            ab[m] = work.tile([P, 2, H], F32, name="ab%d" % m, tag="ab")
-            nc.vector.reciprocal(out=ab[m][:, 0, :], in_=sds[m][:])
-            nc.vector.scalar_tensor_tensor(out=ab[m][:, 1, :], in0=prs[m][:, :, 0], scalar=-0.5, in1=ab[m][:, 0, :], op0=MUL, op1=MUL)
+        def scale_and_shift(m):
+            a_b[m] = work.tile([P, 2, HEADS], F32, name="ab%d" % m, tag="ab")
+            nc.vector.reciprocal(out=a_b[m][:, 0, :], in_=std[m][:])
+            nc.vector.scalar_tensor_tensor(out=a_b[m][:, 1, :], in0=sums[m][:, :, 0], scalar=-0.5, in1=a_b[m][:, 0, :],
+                                           op0=MUL, op1=MUL)
 
-        def prod(m, g):
-            eng = nc.gpsimd if PROD_ON_G[m] else nc.vector
-            if m not in rks:
-                rks[m] = work.tile([P, C], F32, name="rk%d" % m, tag="rk")
-                dd[m] = work.tile([P, H], F32, name="dd%d" % m, tag="dd")
-            cs = slice(512 * g, 512 * g + 512)
-            eng.tensor_tensor(out=rks[m][:, cs], in0=rt[m][:, cs], in1=kt[m][:, cs], op=MUL)
+        def dot_rk(m, g):
+            if g == 0:
+                rkw[m] = work.tile([P, C], F32, name="rkw%d" % m, tag="rkw")
+                dots[m] = work.tile([P, HEADS], F32, name="dot%d" % m, tag="dot")
+            cols = slice(512 * g, 512 * g + 512)
+            nc.vector.tensor_tensor(out=rkw[m][:, cols], in0=r_sb[m][:, cols], in1=k_sb[m][:, cols], op=MUL)
 
-        def prod_b(m, g):
-            cs = slice(512 * g, 512 * g + 512)
-            nc.vector.tensor_tensor(out=rks[m][:, cs], in0=rks[m][:, cs], in1=wb[:, cs], op=MUL)
+        def dot_w(m, g):
+            cols = slice(512 * g, 512 * g + 512)
+            nc.vector.tensor_tensor(out=rkw[m][:, cols], in0=rkw[m][:, cols], in1=rk_all[:, cols], op=MUL)
 
-        def red(m, g):
-            nc.vector.tensor_reduce(out=dd[m][:, 8 * g:8 * g + 8],
-                                    in_=rks[m][:, 512 * g:512 * g + 512].rearrange("t (h i) -> t h i", i=HS),
-                                    axis=AX_X, op=ADD)
+        def dot_sum(m, g):
+            nc.vector.tensor_reduce(out=dots[m][:, 8 * g:8 * g + 8],
+                                    in_=rkw[m][:, 512 * g:512 * g + 512].rearrange("t (h i) -> t h i", i=HEAD),
+                                    axis=AXIS_X, op=ADD)
 
-        def heads_a(j):
-            m, g = divmod(j, 4)
-            s1s[j] = work.tile([P, 4, P], F32, name="s1_%d" % j, tag="s1", bufs=3)
-            for hh in range(8):
-                h = 8 * g + hh
-                u, hq = divmod(hh, 4)
-                if j >= HA_ON_V:
-                    nc.vector.tensor_scalar(out=s1s[j][:, 2 * u:2 * u + 2, 32 * hq:32 * hq + 32],
-                                            in0=yt[m][:, HS * h:HS * h + HS].rearrange("t (p e) -> t e p", e=2),
-                                            scalar1=ab[m][:, 0, h:h + 1], scalar2=ab[m][:, 1, h:h + 1], op0=MUL, op1=ADD)
-                else:
-                    nc.scalar.activation(out=s1s[j][:, 2 * u:2 * u + 2, 32 * hq:32 * hq + 32],
-                                         in_=yt[m][:, HS * h:HS * h + HS].rearrange("t (p e) -> t e p", e=2),
-                                         func=IDENT, bias=ab[m][:, 1, h:h + 1], scale=ab[m][:, 0, h:h + 1])
+        def split_view(tile_ap, h):
+            return tile_ap[:, HEAD * h:HEAD * h + HEAD].rearrange("t (p e) -> t e p", e=2)
 
-        def heads_b(j):
-            m, g = divmod(j, 4)
-            s2s[j] = work.tile([P, 4, P], F32, name="s2_%d" % j, tag="s2", bufs=3)
-            for hh in range(8):
-                h = 8 * g + hh
-                u, hq = divmod(hh, 4)
-                if j >= HB_ON_V:
-                    nc.vector.tensor_scalar(out=s2s[j][:, 2 * u:2 * u + 2, 32 * hq:32 * hq + 32],
-                                            in0=vt[m][:, HS * h:HS * h + HS].rearrange("t (p e) -> t e p", e=2),
-                                            scalar1=dd[m][:, h:h + 1], scalar2=None, op0=MUL)
-                else:
-                    nc.scalar.activation(out=s2s[j][:, 2 * u:2 * u + 2, 32 * hq:32 * hq + 32],
-                                         in_=vt[m][:, HS * h:HS * h + HS].rearrange("t (p e) -> t e p", e=2),
-                                         func=COPY, scale=dd[m][:, h:h + 1])
+        def norm_heads(u):
+            m, g = divmod(u, PASSES)
+            s1[u] = work.tile([P, 4, P], F32, name="s1_%d" % u, tag="s1", bufs=3)
+            for i in range(8):
+                h = 8 * g + i
+                nc.scalar.activation(out=s1[u][:, 2 * (i // 4):2 * (i // 4) + 2, 32 * (i % 4):32 * (i % 4) + 32],
+                                     in_=split_view(y_sb[m], h), func=IDENTITY,
+                                     bias=a_b[m][:, 1, h:h + 1], scale=a_b[m][:, 0, h:h + 1])
 
-        def tr_a(j):
-            pas[j] = psum.tile([P, 4, P], F32, name="pa%d" % j, tag="A", bufs=1)
+        def bonus_heads(u):
+            m, g = divmod(u, PASSES)
+            s2[u] = work.tile([P, 4, P], F32, name="s2_%d" % u, tag="s2", bufs=3)
+            for i in range(8):
+                h = 8 * g + i
+                nc.scalar.activation(out=s2[u][:, 2 * (i // 4):2 * (i // 4) + 2, 32 * (i % 4):32 * (i % 4) + 32],
+                                     in_=split_view(v_sb[m], h), func=COPY, scale=dots[m][:, h:h + 1])
+
+        def turn_s1(u):
+            s1_ps[u] = psum.tile([P, 4, P], F32, name="s1ps%d" % u, tag="A", bufs=1)
             for t in range(4):
-                nc.tensor.transpose(pas[j][:, t, :], s1s[j][:, t, :], ident[:])
+                nc.tensor.transpose(s1_ps[u][:, t, :], s1[u][:, t, :], ident[:])
 
-        def tr_b(j):
-            pbs[j] = psum.tile([P, 4, P], F32, name="pb%d" % j, tag="B", bufs=1)
+        def turn_s2(u):
+            s2_ps[u] = psum.tile([P, 4, P], F32, name="s2ps%d" % u, tag="B", bufs=1)
             for t in range(4):
-                nc.tensor.transpose(pbs[j][:, t, :], s2s[j][:, t, :], ident[:])
+                nc.tensor.transpose(s2_ps[u][:, t, :], s2[u][:, t, :], ident[:])
 
-        def gate(j, t):
-            m, g = divmod(j, 4)
-            if t == 0:
-                pgs[j] = psum.tile([P, 4, P], F32, name="pg%d" % j, tag="G", bufs=1)
-            if True:
-                blk = 4 * g + t
+        def gate(u):
+            m, g = divmod(u, PASSES)
+            gate_ps[u] = psum.tile([P, 4, P], F32, name="gps%d" % u, tag="G", bufs=1)
+            for t in range(4):
+                first = 512 * g + 256 * (t // 2)
                 for e in range(2):
-                    cols = g2s[:, e, 256 * (blk // 2):256 * (blk // 2) + 256].rearrange("q (p f) -> q f p", f=2)[:, blk % 2, :]
-                    nc.tensor.matmul(pgs[j][:, t, :], lhsT=cols, rhs=ghT[:, e, P * m:P * m + P],
+                    every_second = g2_sb[:, e, first:first + 256].rearrange("q (p f) -> q f p", f=2)[:, t % 2, :]
+                    nc.tensor.matmul(gate_ps[u][:, t, :], lhsT=every_second, rhs=gh_t[:, e, P * m:P * m + P],
                                      start=(e == 0), stop=(e == 1))
 
-        def e_one(j):
-            g = j % 4
-            e1s[j] = work.tile([P, 4, P], F32, name="e1_%d" % j, tag="e1", bufs=3)
+        def gain_and_bias(u):
+            g = u % PASSES
+            e1[u] = work.tile([P, 4, P], F32, name="e1_%d" % u, tag="e1", bufs=3)
             for t in range(4):
                 blk = 4 * g + t
-                nc.scalar.activation(out=e1s[j][:, t, :], in_=pas[j][:, t, :], func=IDENT,
-                                     bias=lnT[:, 16 + blk:17 + blk], scale=lnT[:, blk:blk + 1])
+                nc.scalar.activation(out=e1[u][:, t, :], in_=s1_ps[u][:, t, :], func=IDENTITY,
+                                     bias=ln_cols[:, 16 + blk:17 + blk], scale=ln_cols[:, blk:blk + 1])
 
-        def add_(j):
-            nc.vector.tensor_tensor(out=e1s[j][:], in0=e1s[j][:], in1=pbs[j][:], op=ADD)
+        def add_bonus(u):
+            nc.vector.tensor_tensor(out=e1[u][:], in0=e1[u][:], in1=s2_ps[u][:], op=ADD)
 
-        def mul_(j):
-            zgs[j] = work.tile([P, P, 4], BF16, name="zg%d" % j, tag="zg", bufs=3, align_bytes=64)
-            nc.vector.tensor_tensor(out=zgs[j][:], in0=e1s[j][:].rearrange("p t r -> p r t"),
-                                    in1=pgs[j][:].rearrange("p t r -> p r t"), op=MUL)
+        def times_gate(u):
+            z_bf[u] = work.tile([P, P, 4], BF16, name="z%d" % u, tag="z", bufs=3, align_bytes=64)
+            nc.vector.tensor_tensor(out=z_bf[u][:], in0=e1[u][:].rearrange("p t r -> p r t"),
+                                    in1=gate_ps[u][:].rearrange("p t r -> p r t"), op=MUL)
 
-        def zq(j):
-            m, g = divmod(j, 4)
-            nc.vector.quantize_mx(out=zc[:, m, P * g:P * g + P].bitcast(FP8X4), scales=zs[:, m, P * g:P * g + P],
-                                  in_=zgs[j][:].rearrange("p r t -> p (r t)"))
+        def quantise_z(u):
+            m, g = divmod(u, PASSES)
+            nc.vector.quantize_mx(out=z_codes[:, m, P * g:P * g + P].bitcast(FP8X4), scales=z_scales[:, m, P * g:P * g + P],
+                                  in_=z_bf[u][:].rearrange("p r t -> p (r t)"))
 
-        def w_tr(kk):
-            wp, g = divmod(kk, 4)
-            pws[kk] = psum.tile([P, 2, 256], F32, name="pw%d" % kk, tag="X", bufs=5)
-            for u in range(2):
-                for b2 in range(2):
-                    col = 256 * g + 128 * u
-                    nc.tensor.transpose(pws[kk][:, u, P * b2:P * b2 + P], wr[(wp, b2)][:].bitcast(F32)[:, col:col + P], ident[:])
+        def turn_w(pair):
+            for g in range(PASSES):
+                w_ps[(pair, g)] = psum.tile([P, 2, 256], F32, name="wps%d_%d" % (pair, g), tag="X", bufs=5)
+                for half in range(2):
+                    for b in range(2):
+                        col = 256 * g + P * half
+                        nc.tensor.transpose(w_ps[(pair, g)][:, half, P * b:P * b + P],
+                                            w_sb[(pair, b)][:].bitcast(F32)[:, col:col + P], ident[:])
 
-        def w_copy(kk):
-            wp, g = divmod(kk, 4)
-            if g == 0:
-                wgs[wp] = work.tile([P, 4096], BF16, name="wg%d" % wp, tag="wg", bufs=2, align_bytes=64)
-            dst = wgs[wp][:].bitcast(F32).rearrange("p (g c u) -> p g c u", g=NG, u=2)[:, g, :, :]
-            nc.scalar.copy(out=dst, in_=pws[kk][:].rearrange("p u c -> p c u"))
+        def regroup_w(pair):
+            w_bf[pair] = work.tile([P, 4096], BF16, name="wbf%d" % pair, tag="wbf", bufs=2, align_bytes=64)
+            words = w_bf[pair][:].bitcast(F32).rearrange("p (g c u) -> p g c u", g=PASSES, u=2)
+            for g in range(PASSES):
+                nc.scalar.copy(out=words[:, g, :, :], in_=w_ps[(pair, g)][:].rearrange("p u c -> p c u"))
 
-        def w_q(wp):
-            for g in range(NG):
-                nc.vector.quantize_mx(out=wc[:, g, 256 * wp:256 * wp + 256].bitcast(FP8X4), scales=ws[:, g, 256 * wp:256 * wp + 256],
-                                      in_=wgs[wp][:, 1024 * g:1024 * g + 1024])
+        def quantise_w(pair, passes):
+            for g in passes:
+                nc.vector.quantize_mx(out=w_codes[:, g, 256 * pair:256 * pair + 256].bitcast(FP8X4),
+                                      scales=w_scales[:, g, 256 * pair:256 * pair + 256],
+                                      in_=w_bf[pair][:, 1024 * g:1024 * g + 1024])
 
-        def mx_pass(m, n, g):
-            nc.tensor.matmul_mx(out=pos[(m, n)][:], lhsT=zc[:, m, P * g:P * g + P].bitcast(FP8X4), lhsT_scale=zs[:, m, P * g:P * g + P],
-                                rhs=wc[:, g, 512 * n:512 * n + 512].bitcast(FP8X4), rhs_scale=ws[:, g, 512 * n:512 * n + 512],
-                                start=(g == 0), stop=(g == NG - 1))
+        def mx_passes(u):
+            m, g = divmod(u, PASSES)
+            for n in range(4):
+                if g == 0:
+                    out_ps[(m, n)] = psum.tile([P, 512], F32, name="ops%d_%d" % (m, n), tag="X", bufs=5)
+                nc.tensor.matmul_mx(out=out_ps[(m, n)][:],
+                                    lhsT=z_codes[:, m, P * g:P * g + P].bitcast(FP8X4), lhsT_scale=z_scales[:, m, P * g:P * g + P],
+                                    rhs=w_codes[:, g, 512 * n:512 * n + 512].bitcast(FP8X4), rhs_scale=w_scales[:, g, 512 * n:512 * n + 512],
+                                    start=(g == 0), stop=(g == PASSES - 1))
 
-        def drain(m, n):
-            ob = work.tile([P, 512], F32, name="ob%d_%d" % (m, n), tag="ob", bufs=4)
-            if m == NT - 1 and n % 2 == 1:
-                nc.vector.tensor_copy(out=ob[:], in_=pos[(m, n)][:])
-            else:
-                nc.scalar.copy(out=ob[:], in_=pos[(m, n)][:])
-            nc.sync.dma_start(out=out[m, :, 512 * n:512 * n + 512], in_=ob[:])
+        def store_tile(m):
+            for n in range(4):
+                res = work.tile([P, 512], F32, name="res%d_%d" % (m, n), tag="res", bufs=4)
+                if m == TILES - 1 and n % 2 == 1:
+                    nc.vector.tensor_copy(out=res[:], in_=out_ps[(m, n)][:])
+                else:
+                    nc.scalar.copy(out=res[:], in_=out_ps[(m, n)][:])
+                nc.sync.dma_start(out=out[m, :, 512 * n:512 * n + 512], in_=res[:])
 
-        def v_copies(kk):
-            return kk % 4 == 3
+        def is_unit(u):
+            return 0 <= u < UNITS
 
-        def dot2(m, g):
-            prod(m, g)
-            prod(m, g + 1)
-            prod_b(m, g)
-            prod_b(m, g + 1)
-            red(m, g)
-            red(m, g + 1)
-
-        setup_wb((0, 1, 2, 3))
-        bn(0, range(H))
-        stats(0)
-        stats_s(0)
-        stats_b(0)
-        for wp in range(8):
-            for g in range(NG):
-                w_tr(4 * wp + g)
-            if wp == 2:
-                setup_ln_gh()
-            for g in range(NG):
-                w_copy(4 * wp + g)
-            if wp >= 1:
-                w_q(wp - 1)
-            if wp == 0:
-                heads_a(0)
-                heads_a(1)
-            if wp in (0, 1):
-                dot2(0, 2 * wp)
-            if wp == 3:
-                heads_b(0)
-                heads_b(1)
-            if wp in (5, 6):
-                dot2(1, 2 * wp - 10)
-            if wp == 7:
-                bn(1, range(H))
-                stats(1)
-        tr_a(0)
-        tr_b(0)
-        for t in range(4):
-            gate(0, t)
-        w_q(7)
-        e_one(0)
-        stats_s(1)
-
-        tr_a(1)
-        e_one(1)
-        heads_a(2)
-
-        fill = {1: (("bn", 2, 0), ("bn", 2, 1)), 2: (("bn", 2, 2), ("bn", 2, 3), ("sa", 2, 0)), 3: (("pr", 2, 0),),
-                4: (("sb", 2, 0), ("pr", 2, 1)), 5: (("pr", 2, 2), ("bn", 3, 0)), 6: (("pr", 2, 3), ("bn", 3, 1)),
-                7: (("bn", 3, 2), ("bn", 3, 3), ("sa", 3, 0)), 8: (("pr", 3, 0),), 9: (("sb", 3, 0), ("pr", 3, 1)),
-                10: (("pr", 3, 2),), 11: (("pr", 3, 3),)}
-
-        for j in range(0, 17):
-            m, g = divmod(j, 4)
-            todo = fill.get(j, ())
-            if j < 16:
-                add_(j)
-                if j == 0:
-                    stats_b(1)
-                for (kind, fm, part) in todo:
-                    if kind == "sb":
-                        stats_b(fm)
-                    if kind == "bn" and part % 2 == 0:
-                        bn(fm, range(8 * part, 8 * part + 8))
-                    if kind == "pr":
-                        prod(fm, part)
-                mul_(j)
-                for (kind, fm, part) in todo:
-                    if kind == "bn" and part % 2 == 1:
-                        bn(fm, range(8 * part, 8 * part + 8))
-                    if kind == "sa":
-                        stats(fm)
-                    if kind == "pr":
-                        prod_b(fm, part)
-                zq(j)
-                for (kind, fm, part) in todo:
-                    if kind == "pr":
-                        red(fm, part)
-            if j + 1 < 16:
-                tr_b(j + 1)
-                for t in range(4):
-                    gate(j + 1, t)
-            if j + 2 < 16:
-                tr_a(j + 2)
-            if j >= 1:
-                pm, pg_ = divmod(j - 1, 4)
-                for n in range(4):
-                    if pg_ == 0:
-                        pos[(pm, n)] = psum.tile([P, 512], F32, name="po%d_%d" % (pm, n), tag="X", bufs=5)
-                    mx_pass(pm, n, pg_)
-            if j == 16:
-                for n in range(4):
-                    drain(3, n)
-                break
-            for (kind, fm, part) in todo:
-                if kind == "sa":
-                    stats_s(fm)
-            if j + 2 < 16:
-                heads_b(j + 2)
-            if j + 2 < 16:
-                e_one(j + 2)
-            if j + 3 < 16:
-                heads_a(j + 3)
-            if j >= 4 and j % 4 == 0:
-                for n in range(4):
-                    drain(m - 1, n)
+        spread_r_k()
+        for s in range(-9, UNITS + 1):
+            token = [(m, s - (5 * m - 9)) for m in range(TILES) if 0 <= s - (5 * m - 9) < 6]
+            done_pair = s + 7
+            if is_unit(s):
+                add_bonus(s)
+            for (m, t) in token:
+                if t < 2:
+                    bn_part(m, 2 * t)
+                if t == 3:
+                    scale_and_shift(m)
+                if t >= 2:
+                    dot_rk(m, t - 2)
+            if 0 <= done_pair < PAIRS:
+                quantise_w(done_pair, (0, 1))
+            if is_unit(s):
+                times_gate(s)
+            for (m, t) in token:
+                if t < 2:
+                    bn_part(m, 2 * t + 1)
+                if t == 1:
+                    variance(m)
+                if t >= 2:
+                    dot_w(m, t - 2)
+            if 0 <= done_pair < PAIRS:
+                quantise_w(done_pair, (2, 3))
+            if is_unit(s):
+                quantise_z(s)
+            for (m, t) in token:
+                if t >= 2:
+                    dot_sum(m, t - 2)
+            if s == -8:
+                turn_ln_and_g_hid()
+            if 0 <= s + 8 < PAIRS:
+                turn_w(s + 8)
+            if is_unit(s + 1):
+                turn_s2(s + 1)
+                gate(s + 1)
+            if is_unit(s + 2):
+                turn_s1(s + 2)
+            if is_unit(s - 1):
+                mx_passes(s - 1)
+            for (m, t) in token:
+                if t == 2:
+                    root(m)
+            if 0 <= s + 8 < PAIRS:
+                regroup_w(s + 8)
+            if is_unit(s + 2):
+                bonus_heads(s + 2)
+                gain_and_bias(s + 2)
+            if is_unit(s + 3):
+                norm_heads(s + 3)
+            if s >= PASSES and s % PASSES == 0:
+                store_tile(s // PASSES - 1)

@@ -26,6 +26,7 @@ PASSES = 4
 UNITS = TILES * PASSES
 PAIRS = 8
 EPS = 0.00064
+GW = 256
 
 FLOPS = 2 * 512 * 2048 * 2048 + 2 * 512 * 256 * 2048
 
@@ -79,26 +80,26 @@ def tile_full_tmix_params_pc_kernel(tc, y, r, k, v, g_hid, g2, r_k, ln_g, ln_b, 
         nc.sync.dma_start(out=gh_rows[:].rearrange("t (b d) -> t b d", b=TILES), in_=g_hid.rearrange("b t d -> t b d"))
         nc.sync.dma_start(out=lng_rows[0:8, :], in_=ln_g.rearrange("(a b) -> a b", b=2 * P))
         nc.sync.dma_start(out=lnb_rows[0:8, :], in_=ln_b.rearrange("(a b) -> a b", b=2 * P))
-        load_w(0)
         load_rk(0)
+        load_w(0)
         load_w(1)
         load_w(2)
         load_w(3)
         load_y(1)
+        load_rk(1)
         load_w(4)
         load_w(5)
-        load_rk(1)
         load_v(0)
         load_w(6)
         for e in range(2):
             nc.sync.dma_start(out=g2_sb[:, e, :], in_=g2.rearrange("(q e) c -> e q c", e=2)[e])
         load_w(7)
         load_y(2)
-        load_v(1)
         load_rk(2)
+        load_v(1)
         load_y(3)
-        load_v(2)
         load_rk(3)
+        load_v(2)
         load_v(3)
 
         rk_all = const.tile([P, C], BF16, name="rk_all")
@@ -159,16 +160,15 @@ def tile_full_tmix_params_pc_kernel(tc, y, r, k, v, g_hid, g2, r_k, ln_g, ln_b, 
             nc.vector.scalar_tensor_tensor(out=a_b[m][:, 1, :], in0=sums[m][:, :, 0], scalar=-0.5, in1=a_b[m][:, 0, :],
                                            op0=MUL, op1=MUL)
 
-        def dot_rk(m, g):
-            if g == 0:
-                rkw[m] = work.tile([P, C], F32, name="rkw%d" % m, tag="rkw")
-                dots[m] = work.tile([P, HEADS], F32, name="dot%d" % m, tag="dot")
-            cols = slice(512 * g, 512 * g + 512)
-            nc.vector.tensor_tensor(out=rkw[m][:, cols], in0=r_sb[m][:, cols], in1=k_sb[m][:, cols], op=MUL)
-
-        def dot_w(m, g):
-            cols = slice(512 * g, 512 * g + 512)
-            nc.vector.tensor_tensor(out=rkw[m][:, cols], in0=rkw[m][:, cols], in1=rk_all[:, cols], op=MUL)
+        def products(m):
+            rkw[m] = work.tile([P, C], F32, name="rkw%d" % m, tag="rkw")
+            dots[m] = work.tile([P, HEADS], F32, name="dot%d" % m, tag="dot")
+            for first in range(0, C, 2 * GW):
+                both = (slice(first, first + GW), slice(first + GW, first + 2 * GW))
+                for cols in both:
+                    nc.gpsimd.tensor_tensor(out=rkw[m][:, cols], in0=r_sb[m][:, cols], in1=k_sb[m][:, cols], op=MUL)
+                for cols in both:
+                    nc.gpsimd.tensor_tensor(out=rkw[m][:, cols], in0=rkw[m][:, cols], in1=rk_all[:, cols], op=MUL)
 
         def dot_sum(m, g):
             nc.vector.tensor_reduce(out=dots[m][:, 8 * g:8 * g + 8],
@@ -290,8 +290,8 @@ def tile_full_tmix_params_pc_kernel(tc, y, r, k, v, g_hid, g2, r_k, ln_g, ln_b, 
                     bn_part(m, 2 * t)
                 if t == 3:
                     scale_and_shift(m)
-                if t >= 2:
-                    dot_rk(m, t - 2)
+                if t == 0:
+                    products(m)
             if 0 <= done_pair < PAIRS:
                 quantise_w(done_pair, (0, 1))
             if is_unit(s):
@@ -301,8 +301,6 @@ def tile_full_tmix_params_pc_kernel(tc, y, r, k, v, g_hid, g2, r_k, ln_g, ln_b, 
                     bn_part(m, 2 * t + 1)
                 if t == 1:
                     variance(m)
-                if t >= 2:
-                    dot_w(m, t - 2)
             if 0 <= done_pair < PAIRS:
                 quantise_w(done_pair, (2, 3))
             if is_unit(s):

from contextlib import ExitStack

import concourse.mybir as mybir
from concourse.masks import make_identity

F32 = mybir.dt.float32
BF16 = mybir.dt.bfloat16
U32 = mybir.dt.uint32
U8 = mybir.dt.uint8
FP8X4 = mybir.dt.float8_e4m3fn_x4
ADD = mybir.AluOpType.add
SUB = mybir.AluOpType.subtract
MUL = mybir.AluOpType.mult
IDENTITY = mybir.ActivationFunctionType.Identity
COPY = mybir.ActivationFunctionType.Copy
SQRT = mybir.ActivationFunctionType.Sqrt
AXIS_X = mybir.AxisListType.X

P = 128
TILES = 4
C = 2048
CO = 2048
HEAD = 64
HEADS = C // HEAD
PASSES = 4
UNITS = TILES * PASSES
PAIRS = 8
EPS = 0.00064
GW = 256

FLOPS = 2 * 512 * 2048 * 2048 + 2 * 512 * 256 * 2048


def tile_full_tmix_params_pc_kernel(tc, y, r, k, v, g_hid, g2, r_k, ln_g, ln_b, W_o, out):
    nc = tc.nc
    with ExitStack() as ctx:
        const = ctx.enter_context(tc.tile_pool(name="const", bufs=1))
        ld = ctx.enter_context(tc.tile_pool(name="ld", bufs=22))
        work = ctx.enter_context(tc.tile_pool(name="work", bufs=2))
        psum = ctx.enter_context(tc.psum_pool(name="psum", bufs=1))
        ctx.enter_context(tc.manual_schedule())

        ident = const.tile([P, P], F32, name="ident")
        make_identity(nc, ident[:])
        rk_row = ld.tile([P, C], BF16, name="rk_row", tag="ld")
        nc.vector.memset(rk_row[:], 0.0)
        lng_rows = const.tile([P, 2 * P], BF16, name="lng_rows")
        nc.vector.memset(lng_rows[:], 0.0)
        lnb_rows = const.tile([P, 2 * P], BF16, name="lnb_rows")
        nc.vector.memset(lnb_rows[:], 0.0)
        ones = const.tile([P, P], BF16, name="ones")
        nc.vector.memset(ones[:], 1.0)
        gh_rows = const.tile([P, TILES * 256], BF16, name="gh_rows")
        g2_sb = const.tile([P, 2, C], BF16, name="g2_sb")

        y_sb, r_sb, k_sb, v_sb, w_sb = {}, {}, {}, {}, {}

        def load(src, label):
            t = ld.tile([P, C], BF16, name=label, tag="ld")
            nc.sync.dma_start(out=t[:], in_=src)
            return t

        def load_y(m):
            y_sb[m] = load(y[m], "y%d" % m)

        def load_rk(m):
            r_sb[m] = load(r[m], "r%d" % m)
            k_sb[m] = load(k[m], "k%d" % m)

        def load_v(m):
            v_sb[m] = load(v[m], "v%d" % m)

        def load_w(pair):
            for b in range(2):
                row = 256 * pair + P * b
                w_sb[(pair, b)] = load(W_o[row:row + P, :], "w%d_%d" % (pair, b))

        load_y(0)
        nc.sync.dma_start(out=rk_row[0:1, :], in_=r_k.rearrange("(o h) i -> o (h i)", o=1))
        nc.sync.dma_start(out=gh_rows[:].rearrange("t (b d) -> t b d", b=TILES), in_=g_hid.rearrange("b t d -> t b d"))
        nc.sync.dma_start(out=lng_rows[0:8, :], in_=ln_g.rearrange("(a b) -> a b", b=2 * P))
        nc.sync.dma_start(out=lnb_rows[0:8, :], in_=ln_b.rearrange("(a b) -> a b", b=2 * P))
        load_rk(0)
        load_w(0)
        load_w(1)
        load_w(2)
        load_w(3)
        load_y(1)
        load_rk(1)
        load_w(4)
        load_w(5)
        load_v(0)
        load_w(6)
        for e in range(2):
            nc.sync.dma_start(out=g2_sb[:, e, :], in_=g2.rearrange("(q e) c -> e q c", e=2)[e])
        load_w(7)
        load_y(2)
        load_rk(2)
        load_v(1)
        load_y(3)
        load_rk(3)
        load_v(2)
        load_v(3)

        rk_all = const.tile([P, C], BF16, name="rk_all")
        ln_words = const.tile([P, 16], F32, name="ln_words")
        ln_cols = const.tile([P, 32], F32, name="ln_cols")
        gh_t = const.tile([P, 2, 512], BF16, name="gh_t")
        w_codes = const.tile([P, PASSES, CO], U32, name="w_codes", align_bytes=64)
        w_scales = const.tile([P, PASSES, CO], U8, name="w_scales", align_bytes=64)
        z_codes = const.tile([P, TILES, 512], U32, name="z_codes", align_bytes=64)
        z_scales = const.tile([P, TILES, 512], U8, name="z_scales", align_bytes=64)

        def spread_r_k():
            for j in range(4):
                acc = psum.tile([P, 512], F32, name="rk_ps%d" % j, tag=("A", "B", "G", "X")[j], bufs=(1, 1, 1, 5)[j])
                nc.tensor.matmul(acc[:], lhsT=ones[:], rhs=rk_row[:, 512 * j:512 * j + 512], start=True, stop=True)
                nc.scalar.copy(out=rk_all[:, 512 * j:512 * j + 512], in_=acc[:])

        def turn_ln_and_g_hid():
            ln_ps = psum.tile([P, 2, P], F32, name="ln_ps", tag="B", bufs=1)
            nc.tensor.transpose(ln_ps[:, 0, :], lng_rows[:].bitcast(F32), ident[:])
            nc.tensor.transpose(ln_ps[:, 1, :], lnb_rows[:].bitcast(F32), ident[:])
            nc.vector.tensor_copy(out=ln_words[:].rearrange("p (a b) -> p a b", a=2), in_=ln_ps[:, :, 0:8])
            nc.vector.tensor_copy(out=ln_cols[:], in_=ln_words[:].bitcast(BF16))
            gh_ps = psum.tile([P, 512], F32, name="gh_ps", tag="G", bufs=1)
            for m in range(TILES):
                nc.tensor.transpose(gh_ps[:, P * m:P * m + P], gh_rows[:].bitcast(F32)[:, P * m:P * m + P], ident[:])
            nc.vector.tensor_copy(out=gh_t[:], in_=gh_ps[:].bitcast(BF16).rearrange("q (n e) -> q e n", e=2))

        bn_out, sums, var_eps, std, a_b, dots, rkw = {}, {}, {}, {}, {}, {}, {}
        s1, s2, s1_ps, s2_ps, gate_ps, e1, z_bf, w_bf, w_ps, out_ps = {}, {}, {}, {}, {}, {}, {}, {}, {}, {}

        def bn_part(m, part):
            if part == 0:
                bn_out[m] = work.tile([P, HEADS, 6], F32, name="bn%d" % m, tag="bn")
            for h in range(8 * part, 8 * part + 8):
                nc.vector.bn_stats(out=bn_out[m][:, h, :], in_=y_sb[m][:, HEAD * h:HEAD * h + HEAD])

        def variance(m):
            st = bn_out[m]
            sums[m] = work.tile([P, HEADS, 2], F32, name="sums%d" % m, tag="sums")
            nc.vector.tensor_tensor(out=sums[m][:], in0=st[:, :, 1:3], in1=st[:, :, 4:6], op=ADD)
            diff = work.tile([P, HEADS], F32, name="diff%d" % m, tag="diff")
            nc.vector.tensor_tensor(out=diff[:], in0=st[:, :, 1], in1=st[:, :, 4], op=SUB)
            within = work.tile([P, HEADS], F32, name="within%d" % m, tag="within")
            nc.vector.tensor_scalar(out=within[:], in0=sums[m][:, :, 1], scalar1=1.0 / HEAD, scalar2=EPS, op0=MUL, op1=ADD)
            diff2 = work.tile([P, HEADS], F32, name="diffsq%d" % m, tag="diffsq")
            nc.vector.tensor_tensor(out=diff2[:], in0=diff[:], in1=diff[:], op=MUL)
            var_eps[m] = work.tile([P, HEADS], F32, name="vareps%d" % m, tag="vareps")
            nc.vector.scalar_tensor_tensor(out=var_eps[m][:], in0=diff2[:], scalar=0.25, in1=within[:], op0=MUL, op1=ADD)

        def root(m):
            std[m] = work.tile([P, HEADS], F32, name="std%d" % m, tag="std")
            nc.scalar.activation(out=std[m][:], in_=var_eps[m][:], func=SQRT)

        def scale_and_shift(m):
            a_b[m] = work.tile([P, 2, HEADS], F32, name="ab%d" % m, tag="ab")
            nc.vector.reciprocal(out=a_b[m][:, 0, :], in_=std[m][:])
            nc.vector.scalar_tensor_tensor(out=a_b[m][:, 1, :], in0=sums[m][:, :, 0], scalar=-0.5, in1=a_b[m][:, 0, :],
                                           op0=MUL, op1=MUL)

        def products(m):
            rkw[m] = work.tile([P, C], F32, name="rkw%d" % m, tag="rkw")
            dots[m] = work.tile([P, HEADS], F32, name="dot%d" % m, tag="dot")
            for first in range(0, C, 2 * GW):
                both = (slice(first, first + GW), slice(first + GW, first + 2 * GW))
                for cols in both:
                    nc.gpsimd.tensor_tensor(out=rkw[m][:, cols], in0=r_sb[m][:, cols], in1=k_sb[m][:, cols], op=MUL)
                for cols in both:
                    nc.gpsimd.tensor_tensor(out=rkw[m][:, cols], in0=rkw[m][:, cols], in1=rk_all[:, cols], op=MUL)

        def dot_sum(m, g):
            nc.vector.tensor_reduce(out=dots[m][:, 8 * g:8 * g + 8],
                                    in_=rkw[m][:, 512 * g:512 * g + 512].rearrange("t (h i) -> t h i", i=HEAD),
                                    axis=AXIS_X, op=ADD)

        def split_view(tile_ap, h):
            return tile_ap[:, HEAD * h:HEAD * h + HEAD].rearrange("t (p e) -> t e p", e=2)

        def norm_heads(u):
            m, g = divmod(u, PASSES)
            s1[u] = work.tile([P, 4, P], F32, name="s1_%d" % u, tag="s1", bufs=3)
            for i in range(8):
                h = 8 * g + i
                nc.scalar.activation(out=s1[u][:, 2 * (i // 4):2 * (i // 4) + 2, 32 * (i % 4):32 * (i % 4) + 32],
                                     in_=split_view(y_sb[m], h), func=IDENTITY,
                                     bias=a_b[m][:, 1, h:h + 1], scale=a_b[m][:, 0, h:h + 1])

        def bonus_heads(u):
            m, g = divmod(u, PASSES)
            s2[u] = work.tile([P, 4, P], F32, name="s2_%d" % u, tag="s2", bufs=3)
            for i in range(8):
                h = 8 * g + i
                nc.scalar.activation(out=s2[u][:, 2 * (i // 4):2 * (i // 4) + 2, 32 * (i % 4):32 * (i % 4) + 32],
                                     in_=split_view(v_sb[m], h), func=COPY, scale=dots[m][:, h:h + 1])

        def turn_s1(u):
            s1_ps[u] = psum.tile([P, 4, P], F32, name="s1ps%d" % u, tag="A", bufs=1)
            for t in range(4):
                nc.tensor.transpose(s1_ps[u][:, t, :], s1[u][:, t, :], ident[:])

        def turn_s2(u):
            s2_ps[u] = psum.tile([P, 4, P], F32, name="s2ps%d" % u, tag="B", bufs=1)
            for t in range(4):
                nc.tensor.transpose(s2_ps[u][:, t, :], s2[u][:, t, :], ident[:])

        def gate(u):
            m, g = divmod(u, PASSES)
            gate_ps[u] = psum.tile([P, 4, P], F32, name="gps%d" % u, tag="G", bufs=1)
            for t in range(4):
                first = 512 * g + 256 * (t // 2)
                for e in range(2):
                    every_second = g2_sb[:, e, first:first + 256].rearrange("q (p f) -> q f p", f=2)[:, t % 2, :]
                    nc.tensor.matmul(gate_ps[u][:, t, :], lhsT=every_second, rhs=gh_t[:, e, P * m:P * m + P],
                                     start=(e == 0), stop=(e == 1))

        def gain_and_bias(u):
            g = u % PASSES
            e1[u] = work.tile([P, 4, P], F32, name="e1_%d" % u, tag="e1", bufs=3)
            for t in range(4):
                blk = 4 * g + t
                nc.scalar.activation(out=e1[u][:, t, :], in_=s1_ps[u][:, t, :], func=IDENTITY,
                                     bias=ln_cols[:, 16 + blk:17 + blk], scale=ln_cols[:, blk:blk + 1])

        def add_bonus(u):
            nc.vector.tensor_tensor(out=e1[u][:], in0=e1[u][:], in1=s2_ps[u][:], op=ADD)

        def times_gate(u):
            z_bf[u] = work.tile([P, P, 4], BF16, name="z%d" % u, tag="z", bufs=3, align_bytes=64)
            nc.vector.tensor_tensor(out=z_bf[u][:], in0=e1[u][:].rearrange("p t r -> p r t"),
                                    in1=gate_ps[u][:].rearrange("p t r -> p r t"), op=MUL)

        def quantise_z(u):
            m, g = divmod(u, PASSES)
            nc.vector.quantize_mx(out=z_codes[:, m, P * g:P * g + P].bitcast(FP8X4), scales=z_scales[:, m, P * g:P * g + P],
                                  in_=z_bf[u][:].rearrange("p r t -> p (r t)"))

        def turn_w(pair):
            for g in range(PASSES):
                w_ps[(pair, g)] = psum.tile([P, 2, 256], F32, name="wps%d_%d" % (pair, g), tag="X", bufs=5)
                for half in range(2):
                    for b in range(2):
                        col = 256 * g + P * half
                        nc.tensor.transpose(w_ps[(pair, g)][:, half, P * b:P * b + P],
                                            w_sb[(pair, b)][:].bitcast(F32)[:, col:col + P], ident[:])

        def regroup_w(pair):
            w_bf[pair] = work.tile([P, 4096], BF16, name="wbf%d" % pair, tag="wbf", bufs=2, align_bytes=64)
            words = w_bf[pair][:].bitcast(F32).rearrange("p (g c u) -> p g c u", g=PASSES, u=2)
            for g in range(PASSES):
                nc.scalar.copy(out=words[:, g, :, :], in_=w_ps[(pair, g)][:].rearrange("p u c -> p c u"))

        def quantise_w(pair, passes):
            for g in passes:
                nc.vector.quantize_mx(out=w_codes[:, g, 256 * pair:256 * pair + 256].bitcast(FP8X4),
                                      scales=w_scales[:, g, 256 * pair:256 * pair + 256],
                                      in_=w_bf[pair][:, 1024 * g:1024 * g + 1024])

        def mx_passes(u):
            m, g = divmod(u, PASSES)
            for n in range(4):
                if g == 0:
                    out_ps[(m, n)] = psum.tile([P, 512], F32, name="ops%d_%d" % (m, n), tag="X", bufs=5)
                nc.tensor.matmul_mx(out=out_ps[(m, n)][:],
                                    lhsT=z_codes[:, m, P * g:P * g + P].bitcast(FP8X4), lhsT_scale=z_scales[:, m, P * g:P * g + P],
                                    rhs=w_codes[:, g, 512 * n:512 * n + 512].bitcast(FP8X4), rhs_scale=w_scales[:, g, 512 * n:512 * n + 512],
                                    start=(g == 0), stop=(g == PASSES - 1))

        def store_tile(m):
            for n in range(4):
                res = work.tile([P, 512], F32, name="res%d_%d" % (m, n), tag="res", bufs=4)
                if m == TILES - 1 and n % 2 == 1:
                    nc.vector.tensor_copy(out=res[:], in_=out_ps[(m, n)][:])
                else:
                    nc.scalar.copy(out=res[:], in_=out_ps[(m, n)][:])
                nc.sync.dma_start(out=out[m, :, 512 * n:512 * n + 512], in_=res[:])

        def is_unit(u):
            return 0 <= u < UNITS

        spread_r_k()
        for s in range(-9, UNITS + 1):
            token = [(m, s - (5 * m - 9)) for m in range(TILES) if 0 <= s - (5 * m - 9) < 6]
            done_pair = s + 7
            if is_unit(s):
                add_bonus(s)
            for (m, t) in token:
                if t < 2:
                    bn_part(m, 2 * t)
                if t == 3:
                    scale_and_shift(m)
                if t == 0:
                    products(m)
            if 0 <= done_pair < PAIRS:
                quantise_w(done_pair, (0, 1))
            if is_unit(s):
                times_gate(s)
            for (m, t) in token:
                if t < 2:
                    bn_part(m, 2 * t + 1)
                if t == 1:
                    variance(m)
            if 0 <= done_pair < PAIRS:
                quantise_w(done_pair, (2, 3))
            if is_unit(s):
                quantise_z(s)
            for (m, t) in token:
                if t >= 2:
                    dot_sum(m, t - 2)
            if s == -8:
                turn_ln_and_g_hid()
            if 0 <= s + 8 < PAIRS:
                turn_w(s + 8)
            if is_unit(s + 1):
                turn_s2(s + 1)
                gate(s + 1)
            if is_unit(s + 2):
                turn_s1(s + 2)
            if is_unit(s - 1):
                mx_passes(s - 1)
            for (m, t) in token:
                if t == 2:
                    root(m)
            if 0 <= s + 8 < PAIRS:
                regroup_w(s + 8)
            if is_unit(s + 2):
                bonus_heads(s + 2)
                gain_and_bias(s + 2)
            if is_unit(s + 3):
                norm_heads(s + 3)
            if s >= PASSES and s % PASSES == 0:
                store_tile(s // PASSES - 1)
